import numpy as np
import ml_dtypes


def mxq(x, axis, fmt="e4m3"):
    dtype, down = {"e4m3": (ml_dtypes.float8_e4m3fn, 7), "e5m2": (ml_dtypes.float8_e5m2, 14)}[fmt]
    v = np.moveaxis(np.asarray(x, np.float32).astype(ml_dtypes.bfloat16).astype(np.float64), axis, -1)
    blocks = v.reshape(v.shape[:-1] + (-1, 32))
    amax = np.abs(blocks).max(-1, keepdims=True)
    byte = np.maximum(np.where(amax > 0, np.frexp(amax)[1] - 1 + 127, 0) - down, 1)
    scale = np.exp2(byte - 127.0)
    codes = (blocks / scale).astype(np.float32).astype(dtype).astype(np.float64)
    return np.moveaxis((codes * scale).reshape(v.shape), -1, axis)


WIDE = False


def mx_kscale(k):
    if not WIDE:
        return np.ones(k)
    levels = np.array([10, -10, 5, -5, 0])
    a = np.random.permutation(np.resize(levels, k // 512 * 4)).reshape(k // 512, 4)
    idx = np.arange(k)
    return np.exp2(a[idx // 512, idx % 128 // 32])


BF16 = ml_dtypes.bfloat16


def bf(x):
    return np.asarray(x, np.float32).astype(BF16)


def f64(x):
    return np.asarray(x).astype(np.float64)


E2M1 = np.array([0.0, 0.5, 1.0, 1.5, 2.0, 3.0, 4.0, 6.0, -0.0, -0.5, -1.0, -1.5, -2.0, -3.0, -4.0, -6.0])


def pack_weight(w, fmt):
    k, n = w.shape
    w = f64(bf(w)).reshape(k // 32, 32, n)
    amax = np.abs(w).max(1)
    if fmt == "e4m3":
        byte = np.frexp(amax)[1] - 1 + 127 - 7
    else:
        mant, ex = np.frexp(amax / 6.0)
        byte = np.where(mant > 0.5, ex, ex - 1) + 127
    byte = np.clip(np.where(amax > 0, byte, 1), 1, 254)
    scaled = (w * np.exp2(127.0 - byte)[:, None, :]).reshape(k, n).astype(np.float32)
    by_word = np.ascontiguousarray(scaled.reshape(k // 512, 128, 4, n).transpose(0, 1, 3, 2))
    if fmt == "e4m3":
        words = by_word.astype(ml_dtypes.float8_e4m3fn).view(np.uint8)
    else:
        c = by_word.astype(ml_dtypes.float4_e2m1fn).view(np.uint8) & 0xF
        words = c[..., 0::2] | (c[..., 1::2] << 4)
    return np.ascontiguousarray(words), np.ascontiguousarray(byte.astype(np.uint8).reshape(k // 512, 16, n))


def unpack_weight(words, scales, fmt):
    g, p, n, _ = words.shape
    if fmt == "e4m3":
        vals = np.ascontiguousarray(words).view(ml_dtypes.float8_e4m3fn).astype(np.float64)
    else:
        nib = np.empty((g, p, n, 4), np.uint8)
        nib[..., 0::2] = words & 0xF
        nib[..., 1::2] = words >> 4
        vals = E2M1[nib]
    vals = vals * np.repeat(np.exp2(scales.astype(np.float64) - 127.0), 8, axis=1)[..., None]
    return vals.transpose(0, 1, 3, 2).reshape(g * 512, n)

def pack4(w):
    words, scales = pack_weight(w, "e2m1")
    return words.reshape(words.shape[0], 128, -1), scales


def unpack4(words, scales):
    return unpack_weight(words.reshape(words.shape[0], 128, -1, 2), scales, "e2m1")


N, S, D, H, O = 4, 1024, 1024, 512, 1024


def elu(v):
    return np.where(v > 0.0, v, np.exp(np.minimum(v, 0.0)) - 1.0)


def setup_inputs():
    s = mx_kscale(D)
    x = bf(np.random.standard_normal((N, S, D)) * s)
    Wk_words, Wk_scales = pack4(np.random.standard_normal((D, H)) / np.sqrt(D) / s[:, None])
    bk = bf(np.random.standard_normal(H) * 0.1)
    Wv_words, Wv_scales = pack4(np.random.standard_normal((D, H)) / np.sqrt(D) / s[:, None])
    bv = bf(np.random.standard_normal(H) * 0.1)
    return {"x": x,
            "Wk_words": Wk_words,
            "Wk_scales": Wk_scales,
            "bk": bk,
            "Wv_words": Wv_words,
            "Wv_scales": Wv_scales,
            "bv": bv}


def reference(x, Wk_words, Wk_scales, bk, Wv_words, Wv_scales, bv):
    xq = mxq(f64(x), 2, "e4m3")
    keyp = (xq @ unpack4(Wk_words, Wk_scales)) + f64(bk)
    value = (xq @ unpack4(Wv_words, Wv_scales)) + f64(bv)
    K = elu(keyp) + 1.0
    KV = np.sum(K * value, axis=1)
    Ksum = np.sum(K, axis=1)
    return KV, Ksum

@@ -1,0 +1,190 @@
+from contextlib import ExitStack
+
+import concourse.mybir as mybir
+from concourse.masks import make_identity
+
+F32 = mybir.dt.float32
+BF16 = mybir.dt.bfloat16
+I32 = mybir.dt.int32
+U8 = mybir.dt.uint8
+U32 = mybir.dt.uint32
+FP8X4 = mybir.dt.float8_e4m3fn_x4
+FP4X4 = mybir.dt.float4_e2m1fn_x4
+ALU = mybir.AluOpType
+ACT = mybir.ActivationFunctionType
+
+P = 128
+BATCH, SEQ, FEAT, CHAN = 4, 1024, 1024, 512
+K_PASS = 4 * P
+PASSES = FEAT // K_PASS
+CHUNK = 512
+CHUNKS = BATCH * SEQ // CHUNK
+CHUNKS_PER_BATCH = SEQ // CHUNK
+BLOCK = 256
+BLOCKS_PER_CHUNK = CHUNK // BLOCK
+TOKENS_PER_PARTITION = BLOCK // P
+H_TILES = CHAN // P
+UNITS_BEFORE_TRANSPOSES = 2
+
+FLOPS = 2 * BATCH * SEQ * FEAT * 2 * CHAN
+
+
+def tile_linearattention_pa_t_kernel(
+    tc, x, Wk_words, Wk_scales, bk, Wv_words, Wv_scales, bv, out_0, out_1
+):
+    nc = tc.nc
+    with ExitStack() as stack:
+        const = stack.enter_context(tc.tile_pool(name="const", bufs=1))
+        x_pool = stack.enter_context(tc.tile_pool(name="x", bufs=CHUNKS * BLOCKS_PER_CHUNK))
+        grouped_pool = stack.enter_context(tc.tile_pool(name="grouped", bufs=4))
+        codes_pool = stack.enter_context(tc.tile_pool(name="codes", bufs=3))
+        work = stack.enter_context(tc.tile_pool(name="work", bufs=4))
+        psum = stack.enter_context(tc.psum_pool(name="psum", bufs=8))
+
+        w_planes = const.tile([P, 2, PASSES, CHAN], U8, align_bytes=64)
+        nc.vector.memset(w_planes[:].rearrange("p w g n -> p (w g n)").bitcast(I32), 0)
+        bias_rows = const.tile([P, P], BF16)
+        nc.vector.memset(bias_rows[:], 0.0)
+        sums = const.tile([P, P], F32)
+        nc.vector.memset(sums[:], 0.0)
+        ident = const.tile([P, P], F32)
+        make_identity(nc, ident[:])
+
+        x_blocks_dram = x.rearrange(
+            "n (b p t) d -> (n b) p t d", p=P, t=TOKENS_PER_PARTITION
+        )
+        x_blocks = []
+
+        def load_block(b):
+            x_blk = x_pool.tile([P, TOKENS_PER_PARTITION, FEAT], BF16, tag="x")
+            nc.sync.dma_start(out=x_blk[:], in_=x_blocks_dram[b])
+            x_blocks.append(x_blk)
+
+        for b in range(BLOCKS_PER_CHUNK):
+            load_block(b)
+        for w, scales_dram in enumerate((Wk_scales, Wv_scales)):
+            rows = scales_dram.rearrange("g (q r) n -> r q g n", r=4)
+            for r in range(4):
+                nc.sync.dma_start(
+                    out=w_planes[r:P:32, w, :, :].bitcast(I32), in_=rows[r].bitcast(I32)
+                )
+        w_words = []
+        for w, words_dram in enumerate((Wk_words, Wv_words)):
+            words = const.tile([P, PASSES, 2 * CHAN], U8, align_bytes=64, name="words%d" % w)
+            nc.sync.dma_start(
+                out=words[:].bitcast(I32), in_=words_dram.rearrange("g p b -> p g b").bitcast(I32)
+            )
+            w_words.append(words)
+        nc.sync.dma_start(out=bias_rows[0:H_TILES, :], in_=bk.rearrange("(j p) -> j p", p=P))
+        nc.sync.dma_start(out=bias_rows[H_TILES : 2 * H_TILES, :], in_=bv.rearrange("(j p) -> j p", p=P))
+        for b in range(BLOCKS_PER_CHUNK, CHUNKS * BLOCKS_PER_CHUNK):
+            load_block(b)
+
+        kv_parts = const.tile([P, CHUNKS * H_TILES], F32)
+        ksum_parts = const.tile([P, CHUNKS * H_TILES], F32)
+        x_codes = {}
+        x_scales = {}
+
+        def quantise_chunk(c):
+            codes = codes_pool.tile([P, PASSES, CHUNK], U32, align_bytes=64, tag="codes")
+            scales = codes_pool.tile([P, PASSES, CHUNK], U8, align_bytes=64, tag="scales")
+            for blk in range(BLOCKS_PER_CHUNK):
+                x_words = (
+                    x_blocks[c * BLOCKS_PER_CHUNK + blk][:]
+                    .rearrange("p t d -> p (t d)")
+                    .bitcast(F32)
+                    .rearrange("p (t g q u) -> p t g u q", t=TOKENS_PER_PARTITION, g=PASSES, u=2)
+                )
+                cols = slice(blk * BLOCK, (blk + 1) * BLOCK)
+                for g in range(PASSES):
+                    flipped = psum.tile([P, 2, TOKENS_PER_PARTITION, P], F32, tag="bank")
+                    for u in range(2):
+                        for t in range(TOKENS_PER_PARTITION):
+                            nc.tensor.transpose(flipped[:, u, t, :], x_words[:, t, g, u, :], ident[:])
+                    grouped = grouped_pool.tile([P, 4 * BLOCK], BF16, align_bytes=64, tag="grouped")
+                    nc.scalar.copy(
+                        out=grouped[:].bitcast(F32).rearrange("p (c u) -> p c u", u=2),
+                        in_=flipped[:].rearrange("p u t r -> p (t r) u"),
+                    )
+                    nc.vector.quantize_mx(
+                        out=codes[:, g, cols].bitcast(FP8X4), scales=scales[:, g, cols], in_=grouped[:]
+                    )
+            x_codes[c] = codes
+            x_scales[c] = scales
+
+        def product(c, w, j):
+            acc = psum.tile([P, CHUNK], F32, tag="bank")
+            for g in range(PASSES):
+                nc.tensor.matmul_mx(
+                    out=acc[:],
+                    lhsT=w_words[w][:, g, 2 * P * j : 2 * P * (j + 1)].bitcast(FP4X4),
+                    lhsT_scale=w_planes[:, w, g, P * j : P * (j + 1)],
+                    rhs=x_codes[c][:, g, :].bitcast(FP8X4),
+                    rhs_scale=x_scales[c][:, g, :],
+                    start=(g == 0),
+                    stop=(g == PASSES - 1),
+                )
+            return acc
+
+        def unit(c, j):
+            col = (c % CHUNKS_PER_BATCH) * BATCH * H_TILES + (c // CHUNKS_PER_BATCH) * H_TILES + j
+            key_acc = product(c, 0, j)
+            value_acc = product(c, 1, j)
+            grown = work.tile([P, CHUNK], F32, tag="grown")
+            nc.scalar.activation(
+                out=grown[:], in_=key_acc[:], func=ACT.Exp, bias=biases[:, j : j + 1], scale=1.0
+            )
+            nc.gpsimd.tensor_scalar(
+                out=grown[:], in0=grown[:], scalar1=1.0, scalar2=0.0, op0=ALU.min, op1=ALU.max
+            )
+            k_tile = work.tile([P, CHUNK], F32, tag="k")
+            nc.vector.scalar_tensor_tensor(
+                out=k_tile[:],
+                in0=key_acc[:],
+                scalar=bk_plus_1[:, j : j + 1],
+                in1=grown[:],
+                op0=ALU.add,
+                op1=ALU.max,
+                accum_out=ksum_parts[:, col : col + 1],
+            )
+            kv_tile = work.tile([P, CHUNK], F32, tag="kv")
+            nc.vector.scalar_tensor_tensor(
+                out=kv_tile[:],
+                in0=value_acc[:],
+                scalar=biases[:, H_TILES + j : H_TILES + j + 1],
+                in1=k_tile[:],
+                op0=ALU.add,
+                op1=ALU.mult,
+                accum_out=kv_parts[:, col : col + 1],
+            )
+
+        quantise_chunk(0)
+
+        bias_rows_f32 = const.tile([P, P], F32)
+        nc.vector.tensor_copy(out=bias_rows_f32[:], in_=bias_rows[:])
+        bias_flipped = psum.tile([P, P], F32, tag="bank")
+        nc.tensor.transpose(bias_flipped[:], bias_rows_f32[:], ident[:])
+        biases = const.tile([P, 2 * H_TILES], F32)
+        nc.vector.tensor_copy(out=biases[:], in_=bias_flipped[:, 0 : 2 * H_TILES])
+        bk_plus_1 = const.tile([P, H_TILES], F32)
+        nc.vector.tensor_scalar_add(out=bk_plus_1[:], in0=biases[:, 0:H_TILES], scalar1=1.0)
+
+        for c in range(CHUNKS):
+            for j in range(UNITS_BEFORE_TRANSPOSES):
+                unit(c, j)
+            if c + 1 < CHUNKS:
+                quantise_chunk(c + 1)
+            for j in range(UNITS_BEFORE_TRANSPOSES, H_TILES):
+                unit(c, j)
+
+        half = BATCH * H_TILES
+        nc.vector.tensor_add(out=sums[:, 0:half], in0=kv_parts[:, 0:half], in1=kv_parts[:, half : 2 * half])
+        nc.vector.tensor_add(
+            out=sums[:, half : 2 * half], in0=ksum_parts[:, 0:half], in1=ksum_parts[:, half : 2 * half]
+        )
+        sums_flipped = psum.tile([P, P], F32, tag="bank")
+        nc.tensor.transpose(sums_flipped[:], sums[:], ident[:])
+        rows_out = const.tile([P, P], F32)
+        nc.vector.tensor_copy(out=rows_out[:], in_=sums_flipped[:])
+        nc.sync.dma_start(out=out_0.rearrange("n (j p) -> (n j) p", p=P), in_=rows_out[0:half, :])
+        nc.sync.dma_start(out=out_1.rearrange("n (j p) -> (n j) p", p=P), in_=rows_out[half : 2 * half, :])

@@ -134,17 +134,18 @@ def tile_linearattention_pa_t_kernel(
             nc.scalar.activation(
                 out=grown[:], in_=key_acc[:], func=ACT.Exp, bias=biases[:, j : j + 1], scale=1.0
             )
-            nc.gpsimd.tensor_scalar(
-                out=grown[:], in0=grown[:], scalar1=1.0, scalar2=0.0, op0=ALU.min, op1=ALU.max
+            ramp = work.tile([P, CHUNK], F32, tag="ramp")
+            nc.scalar.activation(
+                out=ramp[:], in_=key_acc[:], func=ACT.Relu, bias=biases[:, j : j + 1], scale=1.0
             )
             k_tile = work.tile([P, CHUNK], F32, tag="k")
             nc.vector.scalar_tensor_tensor(
                 out=k_tile[:],
-                in0=key_acc[:],
-                scalar=bk_plus_1[:, j : j + 1],
+                in0=ramp[:],
+                scalar=1.0,
                 in1=grown[:],
                 op0=ALU.add,
-                op1=ALU.max,
+                op1=ALU.min,
                 accum_out=ksum_parts[:, col : col + 1],
             )
             kv_tile = work.tile([P, CHUNK], F32, tag="kv")
@@ -166,8 +167,6 @@ def tile_linearattention_pa_t_kernel(
         nc.tensor.transpose(bias_flipped[:], bias_rows_f32[:], ident[:])
         biases = const.tile([P, 2 * H_TILES], F32)
         nc.vector.tensor_copy(out=biases[:], in_=bias_flipped[:, 0 : 2 * H_TILES])
-        bk_plus_1 = const.tile([P, H_TILES], F32)
-        nc.vector.tensor_scalar_add(out=bk_plus_1[:], in0=biases[:, 0:H_TILES], scalar1=1.0)
 
         for c in range(CHUNKS):
             for j in range(UNITS_BEFORE_TRANSPOSES):

@@ -24,7 +24,7 @@ BLOCK = 256
 BLOCKS_PER_CHUNK = CHUNK // BLOCK
 TOKENS_PER_PARTITION = BLOCK // P
 H_TILES = CHAN // P
-UNITS_BEFORE_TRANSPOSES = 2
+KEY, VALUE = 0, 1
 
 FLOPS = 2 * BATCH * SEQ * FEAT * 2 * CHAN
 
@@ -34,6 +34,7 @@ def tile_linearattention_pa_t_kernel(
 ):
     nc = tc.nc
     with ExitStack() as stack:
+        stack.enter_context(tc.manual_schedule())
         const = stack.enter_context(tc.tile_pool(name="const", bufs=1))
         x_pool = stack.enter_context(tc.tile_pool(name="x", bufs=CHUNKS * BLOCKS_PER_CHUNK))
         grouped_pool = stack.enter_context(tc.tile_pool(name="grouped", bufs=4))
@@ -41,18 +42,16 @@ def tile_linearattention_pa_t_kernel(
         work = stack.enter_context(tc.tile_pool(name="work", bufs=4))
         psum = stack.enter_context(tc.psum_pool(name="psum", bufs=8))
 
-        w_planes = const.tile([P, 2, PASSES, CHAN], U8, align_bytes=64)
-        nc.vector.memset(w_planes[:].rearrange("p w g n -> p (w g n)").bitcast(I32), 0)
         bias_rows = const.tile([P, P], BF16)
         nc.vector.memset(bias_rows[:], 0.0)
+        w_planes = const.tile([P, 2, PASSES, CHAN], U8, align_bytes=64)
+        nc.vector.memset(w_planes[:].rearrange("p w g n -> p (w g n)").bitcast(I32), 0)
         sums = const.tile([P, P], F32)
         nc.vector.memset(sums[:], 0.0)
         ident = const.tile([P, P], F32)
         make_identity(nc, ident[:])
 
-        x_blocks_dram = x.rearrange(
-            "n (b p t) d -> (n b) p t d", p=P, t=TOKENS_PER_PARTITION
-        )
+        x_blocks_dram = x.rearrange("n (b p t) d -> (n b) p t d", p=P, t=TOKENS_PER_PARTITION)
         x_blocks = []
 
         def load_block(b):
@@ -60,23 +59,25 @@ def tile_linearattention_pa_t_kernel(
             nc.sync.dma_start(out=x_blk[:], in_=x_blocks_dram[b])
             x_blocks.append(x_blk)
 
-        for b in range(BLOCKS_PER_CHUNK):
-            load_block(b)
-        for w, scales_dram in enumerate((Wk_scales, Wv_scales)):
+        def load_scales(w, scales_dram):
             rows = scales_dram.rearrange("g (q r) n -> r q g n", r=4)
             for r in range(4):
-                nc.sync.dma_start(
-                    out=w_planes[r:P:32, w, :, :].bitcast(I32), in_=rows[r].bitcast(I32)
-                )
-        w_words = []
-        for w, words_dram in enumerate((Wk_words, Wv_words)):
-            words = const.tile([P, PASSES, 2 * CHAN], U8, align_bytes=64, name="words%d" % w)
+                nc.sync.dma_start(out=w_planes[r:P:32, w, :, :].bitcast(I32), in_=rows[r].bitcast(I32))
+
+        def load_words(name, words_dram):
+            words = const.tile([P, PASSES, 2 * CHAN], U8, align_bytes=64, name=name)
             nc.sync.dma_start(
                 out=words[:].bitcast(I32), in_=words_dram.rearrange("g p b -> p g b").bitcast(I32)
             )
-            w_words.append(words)
+            return words
+
+        for b in range(BLOCKS_PER_CHUNK):
+            load_block(b)
         nc.sync.dma_start(out=bias_rows[0:H_TILES, :], in_=bk.rearrange("(j p) -> j p", p=P))
         nc.sync.dma_start(out=bias_rows[H_TILES : 2 * H_TILES, :], in_=bv.rearrange("(j p) -> j p", p=P))
+        load_scales(KEY, Wk_scales)
+        w_words = [load_words("wk_words", Wk_words), load_words("wv_words", Wv_words)]
+        load_scales(VALUE, Wv_scales)
         for b in range(BLOCKS_PER_CHUNK, CHUNKS * BLOCKS_PER_CHUNK):
             load_block(b)
 
@@ -126,55 +127,62 @@ def tile_linearattention_pa_t_kernel(
                 )
             return acc
 
-        def unit(c, j):
-            col = (c % CHUNKS_PER_BATCH) * BATCH * H_TILES + (c // CHUNKS_PER_BATCH) * H_TILES + j
-            key_acc = product(c, 0, j)
-            value_acc = product(c, 1, j)
-            grown = work.tile([P, CHUNK], F32, tag="grown")
-            nc.scalar.activation(
-                out=grown[:], in_=key_acc[:], func=ACT.Exp, bias=biases[:, j : j + 1], scale=1.0
-            )
-            ramp = work.tile([P, CHUNK], F32, tag="ramp")
-            nc.scalar.activation(
-                out=ramp[:], in_=key_acc[:], func=ACT.Relu, bias=biases[:, j : j + 1], scale=1.0
-            )
-            k_tile = work.tile([P, CHUNK], F32, tag="k")
-            nc.vector.scalar_tensor_tensor(
-                out=k_tile[:],
-                in0=ramp[:],
-                scalar=1.0,
-                in1=grown[:],
-                op0=ALU.add,
-                op1=ALU.min,
-                accum_out=ksum_parts[:, col : col + 1],
-            )
-            kv_tile = work.tile([P, CHUNK], F32, tag="kv")
-            nc.vector.scalar_tensor_tensor(
-                out=kv_tile[:],
-                in0=value_acc[:],
-                scalar=biases[:, H_TILES + j : H_TILES + j + 1],
-                in1=k_tile[:],
-                op0=ALU.add,
-                op1=ALU.mult,
-                accum_out=kv_parts[:, col : col + 1],
-            )
-
-        quantise_chunk(0)
+        def pair(c, tiles):
+            key_accs = {}
+            value_accs = {}
+            grown = {}
+            ramp = {}
+            k_tiles = {}
+            for j in tiles:
+                key_accs[j] = product(c, KEY, j)
+            for j in tiles:
+                value_accs[j] = product(c, VALUE, j)
+            for j in tiles:
+                grown[j] = work.tile([P, CHUNK], F32, tag="grown", name="grown")
+                nc.scalar.activation(
+                    out=grown[j][:], in_=key_accs[j][:], func=ACT.Exp, bias=biases[:, j : j + 1], scale=1.0
+                )
+                ramp[j] = work.tile([P, CHUNK], F32, tag="ramp", name="ramp")
+                nc.scalar.activation(
+                    out=ramp[j][:], in_=key_accs[j][:], func=ACT.Relu, bias=biases[:, j : j + 1], scale=1.0
+                )
+            first_col = (c % CHUNKS_PER_BATCH) * BATCH * H_TILES + (c // CHUNKS_PER_BATCH) * H_TILES
+            for j in tiles:
+                k_tiles[j] = work.tile([P, CHUNK], F32, tag="k", name="k")
+                nc.vector.scalar_tensor_tensor(
+                    out=k_tiles[j][:],
+                    in0=ramp[j][:],
+                    scalar=1.0,
+                    in1=grown[j][:],
+                    op0=ALU.add,
+                    op1=ALU.min,
+                    accum_out=ksum_parts[:, first_col + j : first_col + j + 1],
+                )
+            for j in tiles:
+                kv_tile = work.tile([P, CHUNK], F32, tag="kv")
+                nc.vector.scalar_tensor_tensor(
+                    out=kv_tile[:],
+                    in0=value_accs[j][:],
+                    scalar=biases[:, H_TILES + j : H_TILES + j + 1],
+                    in1=k_tiles[j][:],
+                    op0=ALU.add,
+                    op1=ALU.mult,
+                    accum_out=kv_parts[:, first_col + j : first_col + j + 1],
+                )
 
         bias_rows_f32 = const.tile([P, P], F32)
         nc.vector.tensor_copy(out=bias_rows_f32[:], in_=bias_rows[:])
+        quantise_chunk(0)
         bias_flipped = psum.tile([P, P], F32, tag="bank")
         nc.tensor.transpose(bias_flipped[:], bias_rows_f32[:], ident[:])
         biases = const.tile([P, 2 * H_TILES], F32)
         nc.vector.tensor_copy(out=biases[:], in_=bias_flipped[:, 0 : 2 * H_TILES])
 
         for c in range(CHUNKS):
-            for j in range(UNITS_BEFORE_TRANSPOSES):
-                unit(c, j)
+            pair(c, (0, 1))
             if c + 1 < CHUNKS:
                 quantise_chunk(c + 1)
-            for j in range(UNITS_BEFORE_TRANSPOSES, H_TILES):
-                unit(c, j)
+            pair(c, (2, 3))
 
         half = BATCH * H_TILES
         nc.vector.tensor_add(out=sums[:, 0:half], in0=kv_parts[:, 0:half], in1=kv_parts[:, half : 2 * half])

@@ -29,6 +29,9 @@ KEY, VALUE = 0, 1
 FLOPS = 2 * BATCH * SEQ * FEAT * 2 * CHAN
 
 
+AHEAD = 2
+
+
 def tile_linearattention_pa_t_kernel(
     tc, x, Wk_words, Wk_scales, bk, Wv_words, Wv_scales, bv, out_0, out_1
 ):
@@ -38,8 +41,9 @@ def tile_linearattention_pa_t_kernel(
         const = stack.enter_context(tc.tile_pool(name="const", bufs=1))
         x_pool = stack.enter_context(tc.tile_pool(name="x", bufs=CHUNKS * BLOCKS_PER_CHUNK))
         grouped_pool = stack.enter_context(tc.tile_pool(name="grouped", bufs=4))
-        codes_pool = stack.enter_context(tc.tile_pool(name="codes", bufs=3))
+        codes_pool = stack.enter_context(tc.tile_pool(name="codes", bufs=AHEAD + 2))
         work = stack.enter_context(tc.tile_pool(name="work", bufs=4))
+        k_pool = stack.enter_context(tc.tile_pool(name="k", bufs=2 * H_TILES))
         psum = stack.enter_context(tc.psum_pool(name="psum", bufs=8))
 
         bias_rows = const.tile([P, P], BF16)
@@ -71,24 +75,29 @@ def tile_linearattention_pa_t_kernel(
             )
             return words
 
-        for b in range(BLOCKS_PER_CHUNK):
-            load_block(b)
         nc.sync.dma_start(out=bias_rows[0:H_TILES, :], in_=bk.rearrange("(j p) -> j p", p=P))
         nc.sync.dma_start(out=bias_rows[H_TILES : 2 * H_TILES, :], in_=bv.rearrange("(j p) -> j p", p=P))
+        for b in range(AHEAD * BLOCKS_PER_CHUNK):
+            load_block(b)
         load_scales(KEY, Wk_scales)
         w_words = [load_words("wk_words", Wk_words), load_words("wv_words", Wv_words)]
         load_scales(VALUE, Wv_scales)
-        for b in range(BLOCKS_PER_CHUNK, CHUNKS * BLOCKS_PER_CHUNK):
+        for b in range(AHEAD * BLOCKS_PER_CHUNK, CHUNKS * BLOCKS_PER_CHUNK):
             load_block(b)
 
         kv_parts = const.tile([P, CHUNKS * H_TILES], F32)
         ksum_parts = const.tile([P, CHUNKS * H_TILES], F32)
+        flipped = {}
+        grouped = {}
         x_codes = {}
         x_scales = {}
+        key_accs = {}
+        value_accs = {}
+        clipped = {}
+        k_tiles = {}
+        QUARTERS = BLOCKS_PER_CHUNK * PASSES
 
-        def quantise_chunk(c):
-            codes = codes_pool.tile([P, PASSES, CHUNK], U32, align_bytes=64, tag="codes")
-            scales = codes_pool.tile([P, PASSES, CHUNK], U8, align_bytes=64, tag="scales")
+        def transpose_chunk(c):
             for blk in range(BLOCKS_PER_CHUNK):
                 x_words = (
                     x_blocks[c * BLOCKS_PER_CHUNK + blk][:]
@@ -96,25 +105,36 @@ def tile_linearattention_pa_t_kernel(
                     .bitcast(F32)
                     .rearrange("p (t g q u) -> p t g u q", t=TOKENS_PER_PARTITION, g=PASSES, u=2)
                 )
-                cols = slice(blk * BLOCK, (blk + 1) * BLOCK)
                 for g in range(PASSES):
-                    flipped = psum.tile([P, 2, TOKENS_PER_PARTITION, P], F32, tag="bank")
+                    bank = psum.tile([P, 2, TOKENS_PER_PARTITION, P], F32, tag="bank", name="flipped")
                     for u in range(2):
                         for t in range(TOKENS_PER_PARTITION):
-                            nc.tensor.transpose(flipped[:, u, t, :], x_words[:, t, g, u, :], ident[:])
-                    grouped = grouped_pool.tile([P, 4 * BLOCK], BF16, align_bytes=64, tag="grouped")
-                    nc.scalar.copy(
-                        out=grouped[:].bitcast(F32).rearrange("p (c u) -> p c u", u=2),
-                        in_=flipped[:].rearrange("p u t r -> p (t r) u"),
-                    )
-                    nc.vector.quantize_mx(
-                        out=codes[:, g, cols].bitcast(FP8X4), scales=scales[:, g, cols], in_=grouped[:]
-                    )
+                            nc.tensor.transpose(bank[:, u, t, :], x_words[:, t, g, u, :], ident[:])
+                    flipped[c, blk * PASSES + g] = bank
+
+        def copy_chunk(c):
+            for quarter in range(QUARTERS):
+                laid = grouped_pool.tile([P, 4 * BLOCK], BF16, align_bytes=64, tag="grouped", name="grouped")
+                nc.scalar.copy(
+                    out=laid[:].bitcast(F32).rearrange("p (c u) -> p c u", u=2),
+                    in_=flipped[c, quarter][:].rearrange("p u t r -> p (t r) u"),
+                )
+                grouped[c, quarter] = laid
+
+        def quantise_chunk(c):
+            codes = codes_pool.tile([P, PASSES, CHUNK], U32, align_bytes=64, tag="codes")
+            scales = codes_pool.tile([P, PASSES, CHUNK], U8, align_bytes=64, tag="scales")
+            for quarter in range(QUARTERS):
+                blk, g = quarter // PASSES, quarter % PASSES
+                cols = slice(blk * BLOCK, (blk + 1) * BLOCK)
+                nc.vector.quantize_mx(
+                    out=codes[:, g, cols].bitcast(FP8X4), scales=scales[:, g, cols], in_=grouped[c, quarter][:]
+                )
             x_codes[c] = codes
             x_scales[c] = scales
 
         def product(c, w, j):
-            acc = psum.tile([P, CHUNK], F32, tag="bank")
+            acc = psum.tile([P, CHUNK], F32, tag="bank", name="acc")
             for g in range(PASSES):
                 nc.tensor.matmul_mx(
                     out=acc[:],
@@ -127,62 +147,80 @@ def tile_linearattention_pa_t_kernel(
                 )
             return acc
 
-        def pair(c, tiles):
-            key_accs = {}
-            value_accs = {}
-            grown = {}
-            ramp = {}
-            k_tiles = {}
-            for j in tiles:
-                key_accs[j] = product(c, KEY, j)
-            for j in tiles:
-                value_accs[j] = product(c, VALUE, j)
-            for j in tiles:
-                grown[j] = work.tile([P, CHUNK], F32, tag="grown", name="grown")
+        def keys(c):
+            for j in range(H_TILES):
+                key_accs[c, j] = product(c, KEY, j)
+            for j in range(H_TILES):
+                grown = work.tile([P, CHUNK], F32, tag="grown")
                 nc.scalar.activation(
-                    out=grown[j][:], in_=key_accs[j][:], func=ACT.Exp, bias=biases[:, j : j + 1], scale=1.0
+                    out=grown[:], in_=key_accs[c, j][:], func=ACT.Exp, bias=biases[:, j : j + 1], scale=1.0
                 )
-                ramp[j] = work.tile([P, CHUNK], F32, tag="ramp", name="ramp")
-                nc.scalar.activation(
-                    out=ramp[j][:], in_=key_accs[j][:], func=ACT.Relu, bias=biases[:, j : j + 1], scale=1.0
+                clipped[c, j] = work.tile([P, CHUNK], F32, tag="clipped", name="clipped")
+                nc.gpsimd.tensor_scalar(
+                    out=clipped[c, j][:], in0=grown[:], scalar1=1.0, scalar2=0.0, op0=ALU.min, op1=ALU.max
                 )
-            first_col = (c % CHUNKS_PER_BATCH) * BATCH * H_TILES + (c // CHUNKS_PER_BATCH) * H_TILES
-            for j in tiles:
-                k_tiles[j] = work.tile([P, CHUNK], F32, tag="k", name="k")
-                nc.vector.scalar_tensor_tensor(
-                    out=k_tiles[j][:],
-                    in0=ramp[j][:],
-                    scalar=1.0,
-                    in1=grown[j][:],
-                    op0=ALU.add,
-                    op1=ALU.min,
-                    accum_out=ksum_parts[:, first_col + j : first_col + j + 1],
-                )
-            for j in tiles:
-                kv_tile = work.tile([P, CHUNK], F32, tag="kv")
-                nc.vector.scalar_tensor_tensor(
-                    out=kv_tile[:],
-                    in0=value_accs[j][:],
-                    scalar=biases[:, H_TILES + j : H_TILES + j + 1],
-                    in1=k_tiles[j][:],
-                    op0=ALU.add,
-                    op1=ALU.mult,
-                    accum_out=kv_parts[:, first_col + j : first_col + j + 1],
-                )
+
+        def part_col(c, j):
+            return (c % CHUNKS_PER_BATCH) * BATCH * H_TILES + (c // CHUNKS_PER_BATCH) * H_TILES + j
+
+        def k_of(c, j):
+            k_tiles[c, j] = k_pool.tile([P, CHUNK], F32, tag="k", name="k")
+            nc.vector.scalar_tensor_tensor(
+                out=k_tiles[c, j][:],
+                in0=key_accs[c, j][:],
+                scalar=biases[:, 2 * H_TILES + j : 2 * H_TILES + j + 1],
+                in1=clipped[c, j][:],
+                op0=ALU.add,
+                op1=ALU.max,
+                accum_out=ksum_parts[:, part_col(c, j) : part_col(c, j) + 1],
+            )
+
+        def kv_of(c, j):
+            kv_tile = work.tile([P, CHUNK], F32, tag="kv")
+            nc.vector.scalar_tensor_tensor(
+                out=kv_tile[:],
+                in0=value_accs[c, j][:],
+                scalar=biases[:, H_TILES + j : H_TILES + j + 1],
+                in1=k_tiles[c, j][:],
+                op0=ALU.add,
+                op1=ALU.mult,
+                accum_out=kv_parts[:, part_col(c, j) : part_col(c, j) + 1],
+            )
 
         bias_rows_f32 = const.tile([P, P], F32)
         nc.vector.tensor_copy(out=bias_rows_f32[:], in_=bias_rows[:])
+        transpose_chunk(0)
+        copy_chunk(0)
         quantise_chunk(0)
         bias_flipped = psum.tile([P, P], F32, tag="bank")
         nc.tensor.transpose(bias_flipped[:], bias_rows_f32[:], ident[:])
-        biases = const.tile([P, 2 * H_TILES], F32)
-        nc.vector.tensor_copy(out=biases[:], in_=bias_flipped[:, 0 : 2 * H_TILES])
+        biases = const.tile([P, 3 * H_TILES], F32)
+        nc.vector.tensor_copy(out=biases[:, 0 : 2 * H_TILES], in_=bias_flipped[:, 0 : 2 * H_TILES])
+        nc.vector.tensor_scalar_add(
+            out=biases[:, 2 * H_TILES : 3 * H_TILES], in0=bias_flipped[:, 0:H_TILES], scalar1=1.0
+        )
+        for c in range(1, AHEAD):
+            transpose_chunk(c)
+            copy_chunk(c)
+            quantise_chunk(c)
+        keys(0)
+        k_of(0, 0)
 
         for c in range(CHUNKS):
-            pair(c, (0, 1))
+            if c + AHEAD < CHUNKS:
+                transpose_chunk(c + AHEAD)
+                copy_chunk(c + AHEAD)
+            for j in range(1, H_TILES):
+                k_of(c, j)
+            if c + AHEAD < CHUNKS:
+                quantise_chunk(c + AHEAD)
+            for j in range(H_TILES):
+                value_accs[c, j] = product(c, VALUE, j)
+            for j in range(H_TILES):
+                kv_of(c, j)
             if c + 1 < CHUNKS:
-                quantise_chunk(c + 1)
-            pair(c, (2, 3))
+                keys(c + 1)
+                k_of(c + 1, 0)
 
         half = BATCH * H_TILES
         nc.vector.tensor_add(out=sums[:, 0:half], in0=kv_parts[:, 0:half], in1=kv_parts[:, half : 2 * half])

@@ -30,6 +30,7 @@ FLOPS = 2 * BATCH * SEQ * FEAT * 2 * CHAN
 
 
 AHEAD = 2
+SORTED_BLOCKS = 1
 
 
 def tile_linearattention_pa_t_kernel(
@@ -44,6 +45,7 @@ def tile_linearattention_pa_t_kernel(
         codes_pool = stack.enter_context(tc.tile_pool(name="codes", bufs=AHEAD + 2))
         work = stack.enter_context(tc.tile_pool(name="work", bufs=4))
         k_pool = stack.enter_context(tc.tile_pool(name="k", bufs=2 * H_TILES))
+        sorted_pool = stack.enter_context(tc.tile_pool(name="sorted", bufs=2 * SORTED_BLOCKS))
         psum = stack.enter_context(tc.psum_pool(name="psum", bufs=8))
 
         bias_rows = const.tile([P, P], BF16)
@@ -54,6 +56,8 @@ def tile_linearattention_pa_t_kernel(
         nc.vector.memset(sums[:], 0.0)
         ident = const.tile([P, P], F32)
         make_identity(nc, ident[:])
+        warm = const.tile([P, 1], F32)
+        nc.scalar.activation(out=warm[:], in_=sums[:, 0:1], func=ACT.Exp)
 
         x_blocks_dram = x.rearrange("n (b p t) d -> (n b) p t d", p=P, t=TOKENS_PER_PARTITION)
         x_blocks = []
@@ -85,8 +89,7 @@ def tile_linearattention_pa_t_kernel(
         for b in range(AHEAD * BLOCKS_PER_CHUNK, CHUNKS * BLOCKS_PER_CHUNK):
             load_block(b)
 
-        kv_parts = const.tile([P, CHUNKS * H_TILES], F32)
-        ksum_parts = const.tile([P, CHUNKS * H_TILES], F32)
+        parts = const.tile([P, CHUNKS_PER_BATCH, 2, BATCH, H_TILES], F32)
         flipped = {}
         grouped = {}
         x_codes = {}
@@ -97,14 +100,31 @@ def tile_linearattention_pa_t_kernel(
         k_tiles = {}
         QUARTERS = BLOCKS_PER_CHUNK * PASSES
 
+        sorted_words = {}
+
+        def sort_chunk(c):
+            for blk in range(SORTED_BLOCKS):
+                b = c * BLOCKS_PER_CHUNK + blk
+                sorted_words[b] = sorted_pool.tile([P, BLOCK * FEAT // (2 * P)], F32, tag="sorted", name="sorted")
+                nc.gpsimd.tensor_copy(
+                    out=sorted_words[b][:].rearrange("p (a u q) -> p a u q", u=2, q=P),
+                    in_=x_blocks[b][:].rearrange("p t d -> p (t d)").bitcast(F32).rearrange("p (a q u) -> p a u q", u=2, q=P),
+                )
+
         def transpose_chunk(c):
             for blk in range(BLOCKS_PER_CHUNK):
-                x_words = (
-                    x_blocks[c * BLOCKS_PER_CHUNK + blk][:]
-                    .rearrange("p t d -> p (t d)")
-                    .bitcast(F32)
-                    .rearrange("p (t g q u) -> p t g u q", t=TOKENS_PER_PARTITION, g=PASSES, u=2)
-                )
+                b = c * BLOCKS_PER_CHUNK + blk
+                if b in sorted_words:
+                    x_words = sorted_words[b][:].rearrange(
+                        "p (t g u q) -> p t g u q", t=TOKENS_PER_PARTITION, g=PASSES, u=2
+                    )
+                else:
+                    x_words = (
+                        x_blocks[b][:]
+                        .rearrange("p t d -> p (t d)")
+                        .bitcast(F32)
+                        .rearrange("p (t g q u) -> p t g u q", t=TOKENS_PER_PARTITION, g=PASSES, u=2)
+                    )
                 for g in range(PASSES):
                     bank = psum.tile([P, 2, TOKENS_PER_PARTITION, P], F32, tag="bank", name="flipped")
                     for u in range(2):
@@ -160,9 +180,6 @@ def tile_linearattention_pa_t_kernel(
                     out=clipped[c, j][:], in0=grown[:], scalar1=1.0, scalar2=0.0, op0=ALU.min, op1=ALU.max
                 )
 
-        def part_col(c, j):
-            return (c % CHUNKS_PER_BATCH) * BATCH * H_TILES + (c // CHUNKS_PER_BATCH) * H_TILES + j
-
         def k_of(c, j):
             k_tiles[c, j] = k_pool.tile([P, CHUNK], F32, tag="k", name="k")
             nc.vector.scalar_tensor_tensor(
@@ -172,7 +189,7 @@ def tile_linearattention_pa_t_kernel(
                 in1=clipped[c, j][:],
                 op0=ALU.add,
                 op1=ALU.max,
-                accum_out=ksum_parts[:, part_col(c, j) : part_col(c, j) + 1],
+                accum_out=parts[:, c % CHUNKS_PER_BATCH, 1, c // CHUNKS_PER_BATCH, j : j + 1],
             )
 
         def kv_of(c, j):
@@ -184,7 +201,7 @@ def tile_linearattention_pa_t_kernel(
                 in1=k_tiles[c, j][:],
                 op0=ALU.add,
                 op1=ALU.mult,
-                accum_out=kv_parts[:, part_col(c, j) : part_col(c, j) + 1],
+                accum_out=parts[:, c % CHUNKS_PER_BATCH, 0, c // CHUNKS_PER_BATCH, j : j + 1],
             )
 
         bias_rows_f32 = const.tile([P, P], F32)
@@ -221,15 +238,18 @@ def tile_linearattention_pa_t_kernel(
             if c + 1 < CHUNKS:
                 keys(c + 1)
                 k_of(c + 1, 0)
+            if c + AHEAD + 1 < CHUNKS:
+                sort_chunk(c + AHEAD + 1)
 
         half = BATCH * H_TILES
-        nc.vector.tensor_add(out=sums[:, 0:half], in0=kv_parts[:, 0:half], in1=kv_parts[:, half : 2 * half])
         nc.vector.tensor_add(
-            out=sums[:, half : 2 * half], in0=ksum_parts[:, 0:half], in1=ksum_parts[:, half : 2 * half]
+            out=sums[:, 0 : 2 * half],
+            in0=parts[:, 0, :, :, :].rearrange("p s n j -> p (s n j)"),
+            in1=parts[:, 1, :, :, :].rearrange("p s n j -> p (s n j)"),
         )
         sums_flipped = psum.tile([P, P], F32, tag="bank")
         nc.tensor.transpose(sums_flipped[:], sums[:], ident[:])
         rows_out = const.tile([P, P], F32)
         nc.vector.tensor_copy(out=rows_out[:], in_=sums_flipped[:])
         nc.sync.dma_start(out=out_0.rearrange("n (j p) -> (n j) p", p=P), in_=rows_out[0:half, :])
-        nc.sync.dma_start(out=out_1.rearrange("n (j p) -> (n j) p", p=P), in_=rows_out[half : 2 * half, :])
+        nc.scalar.dma_start(out=out_1.rearrange("n (j p) -> (n j) p", p=P), in_=rows_out[half : 2 * half, :])

@@ -30,7 +30,7 @@ FLOPS = 2 * BATCH * SEQ * FEAT * 2 * CHAN
 
 
 AHEAD = 2
-SORTED_BLOCKS = 1
+SORTED_BLOCKS = 2
 
 
 def tile_linearattention_pa_t_kernel(
@@ -227,19 +227,26 @@ def tile_linearattention_pa_t_kernel(
             if c + AHEAD < CHUNKS:
                 transpose_chunk(c + AHEAD)
                 copy_chunk(c + AHEAD)
-            for j in range(1, H_TILES):
-                k_of(c, j)
             if c + AHEAD < CHUNKS:
+                for j in range(1, H_TILES):
+                    k_of(c, j)
                 quantise_chunk(c + AHEAD)
-            for j in range(H_TILES):
-                value_accs[c, j] = product(c, VALUE, j)
-            for j in range(H_TILES):
-                kv_of(c, j)
+                if c + AHEAD + 1 < CHUNKS:
+                    sort_chunk(c + AHEAD + 1)
+                for j in range(H_TILES):
+                    value_accs[c, j] = product(c, VALUE, j)
+                for j in range(H_TILES):
+                    kv_of(c, j)
+            else:
+                value_accs[c, 0] = product(c, VALUE, 0)
+                for j in range(1, H_TILES):
+                    k_of(c, j)
+                    value_accs[c, j] = product(c, VALUE, j)
+                    kv_of(c, j - 1)
+                kv_of(c, H_TILES - 1)
             if c + 1 < CHUNKS:
                 keys(c + 1)
                 k_of(c + 1, 0)
-            if c + AHEAD + 1 < CHUNKS:
-                sort_chunk(c + AHEAD + 1)
 
         half = BATCH * H_TILES
         nc.vector.tensor_add(

@@ -30,7 +30,7 @@ FLOPS = 2 * BATCH * SEQ * FEAT * 2 * CHAN
 
 
 AHEAD = 2
-SORTED_BLOCKS = 2
+SORTED_BLOCKS = 1
 
 
 def tile_linearattention_pa_t_kernel(
@@ -106,7 +106,7 @@ def tile_linearattention_pa_t_kernel(
             for blk in range(SORTED_BLOCKS):
                 b = c * BLOCKS_PER_CHUNK + blk
                 sorted_words[b] = sorted_pool.tile([P, BLOCK * FEAT // (2 * P)], F32, tag="sorted", name="sorted")
-                nc.gpsimd.tensor_copy(
+                nc.scalar.copy(
                     out=sorted_words[b][:].rearrange("p (a u q) -> p a u q", u=2, q=P),
                     in_=x_blocks[b][:].rearrange("p t d -> p (t d)").bitcast(F32).rearrange("p (a q u) -> p a u q", u=2, q=P),
                 )

@@ -12,6 +12,7 @@ FP8X4 = mybir.dt.float8_e4m3fn_x4
 FP4X4 = mybir.dt.float4_e2m1fn_x4
 ALU = mybir.AluOpType
 ACT = mybir.ActivationFunctionType
+AX = mybir.AxisListType
 
 P = 128
 BATCH, SEQ, FEAT, CHAN = 4, 1024, 1024, 512
@@ -30,7 +31,8 @@ FLOPS = 2 * BATCH * SEQ * FEAT * 2 * CHAN
 
 
 AHEAD = 2
-SORTED_BLOCKS = 1
+SUMMED_CHUNKS = 2
+TERMS = 2 * CHUNKS_PER_BATCH
 
 
 def tile_linearattention_pa_t_kernel(
@@ -45,7 +47,7 @@ def tile_linearattention_pa_t_kernel(
         codes_pool = stack.enter_context(tc.tile_pool(name="codes", bufs=AHEAD + 2))
         work = stack.enter_context(tc.tile_pool(name="work", bufs=4))
         k_pool = stack.enter_context(tc.tile_pool(name="k", bufs=2 * H_TILES))
-        sorted_pool = stack.enter_context(tc.tile_pool(name="sorted", bufs=2 * SORTED_BLOCKS))
+        sorted_pool = stack.enter_context(tc.tile_pool(name="sorted", bufs=2 * BLOCKS_PER_CHUNK))
         psum = stack.enter_context(tc.psum_pool(name="psum", bufs=8))
 
         bias_rows = const.tile([P, P], BF16)
@@ -84,12 +86,19 @@ def tile_linearattention_pa_t_kernel(
         for b in range(AHEAD * BLOCKS_PER_CHUNK):
             load_block(b)
         load_scales(KEY, Wk_scales)
-        w_words = [load_words("wk_words", Wk_words), load_words("wv_words", Wv_words)]
+        w_words = [load_words("wk_words", Wk_words)]
+        for b in range(AHEAD * BLOCKS_PER_CHUNK, (AHEAD + 1) * BLOCKS_PER_CHUNK):
+            load_block(b)
+        w_words.append(load_words("wv_words", Wv_words))
         load_scales(VALUE, Wv_scales)
-        for b in range(AHEAD * BLOCKS_PER_CHUNK, CHUNKS * BLOCKS_PER_CHUNK):
+        for b in range((AHEAD + 1) * BLOCKS_PER_CHUNK, CHUNKS * BLOCKS_PER_CHUNK):
             load_block(b)
 
-        parts = const.tile([P, CHUNKS_PER_BATCH, 2, BATCH, H_TILES], F32)
+        parts = const.tile([P, TERMS, 2, BATCH, H_TILES], F32)
+        nc.vector.memset(parts[:].rearrange("p t s n j -> p (t s n j)"), 0.0)
+
+        def summed(c, j):
+            return c >= CHUNKS - SUMMED_CHUNKS and j == H_TILES - 1
         flipped = {}
         grouped = {}
         x_codes = {}
@@ -102,14 +111,16 @@ def tile_linearattention_pa_t_kernel(
 
         sorted_words = {}
 
+        def sort_block(b, copy):
+            sorted_words[b] = sorted_pool.tile([P, BLOCK * FEAT // (2 * P)], F32, tag="sorted", name="sorted")
+            copy(
+                out=sorted_words[b][:].rearrange("p (a u q) -> p a u q", u=2, q=P),
+                in_=x_blocks[b][:].rearrange("p t d -> p (t d)").bitcast(F32).rearrange("p (a q u) -> p a u q", u=2, q=P),
+            )
+
         def sort_chunk(c):
-            for blk in range(SORTED_BLOCKS):
-                b = c * BLOCKS_PER_CHUNK + blk
-                sorted_words[b] = sorted_pool.tile([P, BLOCK * FEAT // (2 * P)], F32, tag="sorted", name="sorted")
-                nc.scalar.copy(
-                    out=sorted_words[b][:].rearrange("p (a u q) -> p a u q", u=2, q=P),
-                    in_=x_blocks[b][:].rearrange("p t d -> p (t d)").bitcast(F32).rearrange("p (a q u) -> p a u q", u=2, q=P),
-                )
+            sort_block(c * BLOCKS_PER_CHUNK, nc.scalar.copy)
+            sort_block(c * BLOCKS_PER_CHUNK + 1, nc.gpsimd.tensor_copy)
 
         def transpose_chunk(c):
             for blk in range(BLOCKS_PER_CHUNK):
@@ -167,10 +178,39 @@ def tile_linearattention_pa_t_kernel(
                 )
             return acc
 
+        def k_as_sum(c, j):
+            term, n = c % CHUNKS_PER_BATCH, c // CHUNKS_PER_BATCH
+            fallen = work.tile([P, CHUNK], F32, tag="fallen")
+            nc.scalar.activation(
+                out=fallen[:],
+                in_=key_accs[c, j][:],
+                func=ACT.Relu,
+                bias=biases[:, 3 * H_TILES + j : 3 * H_TILES + j + 1],
+                scale=-1.0,
+            )
+            ramp = work.tile([P, CHUNK], F32, tag="ramp")
+            nc.scalar.activation(
+                out=ramp[:],
+                in_=key_accs[c, j][:],
+                func=ACT.Relu,
+                bias=biases[:, j : j + 1],
+                scale=1.0,
+                accum_out=parts[:, CHUNKS_PER_BATCH + term, 1, n, j : j + 1],
+            )
+            decayed = work.tile([P, CHUNK], F32, tag="decayed")
+            nc.scalar.activation(
+                out=decayed[:], in_=fallen[:], func=ACT.Exp, scale=-1.0, accum_out=parts[:, term, 1, n, j : j + 1]
+            )
+            k_tiles[c, j] = k_pool.tile([P, CHUNK], F32, tag="k", name="k")
+            nc.gpsimd.tensor_tensor(out=k_tiles[c, j][:], in0=decayed[:], in1=ramp[:], op=ALU.add)
+
         def keys(c):
             for j in range(H_TILES):
                 key_accs[c, j] = product(c, KEY, j)
             for j in range(H_TILES):
+                if summed(c, j):
+                    k_as_sum(c, j)
+                    continue
                 grown = work.tile([P, CHUNK], F32, tag="grown")
                 nc.scalar.activation(
                     out=grown[:], in_=key_accs[c, j][:], func=ACT.Exp, bias=biases[:, j : j + 1], scale=1.0
@@ -181,6 +221,8 @@ def tile_linearattention_pa_t_kernel(
                 )
 
         def k_of(c, j):
+            if summed(c, j):
+                return
             k_tiles[c, j] = k_pool.tile([P, CHUNK], F32, tag="k", name="k")
             nc.vector.scalar_tensor_tensor(
                 out=k_tiles[c, j][:],
@@ -211,15 +253,20 @@ def tile_linearattention_pa_t_kernel(
         quantise_chunk(0)
         bias_flipped = psum.tile([P, P], F32, tag="bank")
         nc.tensor.transpose(bias_flipped[:], bias_rows_f32[:], ident[:])
-        biases = const.tile([P, 3 * H_TILES], F32)
+        biases = const.tile([P, 4 * H_TILES], F32)
         nc.vector.tensor_copy(out=biases[:, 0 : 2 * H_TILES], in_=bias_flipped[:, 0 : 2 * H_TILES])
         nc.vector.tensor_scalar_add(
             out=biases[:, 2 * H_TILES : 3 * H_TILES], in0=bias_flipped[:, 0:H_TILES], scalar1=1.0
+        )
+        nc.vector.tensor_scalar_mul(
+            out=biases[:, 3 * H_TILES : 4 * H_TILES], in0=bias_flipped[:, 0:H_TILES], scalar1=-1.0
         )
         for c in range(1, AHEAD):
             transpose_chunk(c)
             copy_chunk(c)
             quantise_chunk(c)
+        for blk in range(BLOCKS_PER_CHUNK):
+            sort_block(AHEAD * BLOCKS_PER_CHUNK + blk, nc.vector.tensor_copy)
         keys(0)
         k_of(0, 0)
 
@@ -230,12 +277,14 @@ def tile_linearattention_pa_t_kernel(
             if c + AHEAD < CHUNKS:
                 for j in range(1, H_TILES):
                     k_of(c, j)
-                quantise_chunk(c + AHEAD)
                 if c + AHEAD + 1 < CHUNKS:
                     sort_chunk(c + AHEAD + 1)
                 for j in range(H_TILES):
                     value_accs[c, j] = product(c, VALUE, j)
-                for j in range(H_TILES):
+                for j in range(H_TILES // 2):
+                    kv_of(c, j)
+                quantise_chunk(c + AHEAD)
+                for j in range(H_TILES // 2, H_TILES):
                     kv_of(c, j)
             else:
                 value_accs[c, 0] = product(c, VALUE, 0)
@@ -249,10 +298,8 @@ def tile_linearattention_pa_t_kernel(
                 k_of(c + 1, 0)
 
         half = BATCH * H_TILES
-        nc.vector.tensor_add(
-            out=sums[:, 0 : 2 * half],
-            in0=parts[:, 0, :, :, :].rearrange("p s n j -> p (s n j)"),
-            in1=parts[:, 1, :, :, :].rearrange("p s n j -> p (s n j)"),
+        nc.vector.tensor_reduce(
+            out=sums[:, 0 : 2 * half], in_=parts[:].rearrange("p t s n j -> p (s n j) t"), axis=AX.X, op=ALU.add
         )
         sums_flipped = psum.tile([P, P], F32, tag="bank")
         nc.tensor.transpose(sums_flipped[:], sums[:], ident[:])

@@ -52,7 +52,7 @@ def tile_linearattention_pa_t_kernel(
 
         bias_rows = const.tile([P, P], BF16)
         nc.vector.memset(bias_rows[:], 0.0)
-        w_planes = const.tile([P, 2, PASSES, CHAN], U8, align_bytes=64)
+        w_planes = const.tile([P, 2, PASSES, CHAN], U8, align_bytes=256)
         nc.vector.memset(w_planes[:].rearrange("p w g n -> p (w g n)").bitcast(I32), 0)
         sums = const.tile([P, P], F32)
         nc.vector.memset(sums[:], 0.0)
@@ -75,7 +75,7 @@ def tile_linearattention_pa_t_kernel(
                 nc.sync.dma_start(out=w_planes[r:P:32, w, :, :].bitcast(I32), in_=rows[r].bitcast(I32))
 
         def load_words(name, words_dram):
-            words = const.tile([P, PASSES, 2 * CHAN], U8, align_bytes=64, name=name)
+            words = const.tile([P, PASSES, 2 * CHAN], U8, align_bytes=256, name=name)
             nc.sync.dma_start(
                 out=words[:].bitcast(I32), in_=words_dram.rearrange("g p b -> p g b").bitcast(I32)
             )
@@ -153,8 +153,8 @@ def tile_linearattention_pa_t_kernel(
                 grouped[c, quarter] = laid
 
         def quantise_chunk(c):
-            codes = codes_pool.tile([P, PASSES, CHUNK], U32, align_bytes=64, tag="codes")
-            scales = codes_pool.tile([P, PASSES, CHUNK], U8, align_bytes=64, tag="scales")
+            codes = codes_pool.tile([P, PASSES, CHUNK], U32, align_bytes=256, tag="codes")
+            scales = codes_pool.tile([P, PASSES, CHUNK], U8, align_bytes=256, tag="scales")
             for quarter in range(QUARTERS):
                 blk, g = quarter // PASSES, quarter % PASSES
                 cols = slice(blk * BLOCK, (blk + 1) * BLOCK)

@@ -12,7 +12,6 @@ FP8X4 = mybir.dt.float8_e4m3fn_x4
 FP4X4 = mybir.dt.float4_e2m1fn_x4
 ALU = mybir.AluOpType
 ACT = mybir.ActivationFunctionType
-AX = mybir.AxisListType
 
 P = 128
 BATCH, SEQ, FEAT, CHAN = 4, 1024, 1024, 512
@@ -26,6 +25,7 @@ BLOCKS_PER_CHUNK = CHUNK // BLOCK
 TOKENS_PER_PARTITION = BLOCK // P
 H_TILES = CHAN // P
 KEY, VALUE = 0, 1
+KV, KSUM = 0, 1
 
 FLOPS = 2 * BATCH * SEQ * FEAT * 2 * CHAN
 
@@ -43,23 +43,23 @@ def tile_linearattention_pa_t_kernel(
         stack.enter_context(tc.manual_schedule())
         const = stack.enter_context(tc.tile_pool(name="const", bufs=1))
         x_pool = stack.enter_context(tc.tile_pool(name="x", bufs=CHUNKS * BLOCKS_PER_CHUNK))
-        grouped_pool = stack.enter_context(tc.tile_pool(name="grouped", bufs=4))
+        grouped_pool = stack.enter_context(tc.tile_pool(name="grouped", bufs=2))
         codes_pool = stack.enter_context(tc.tile_pool(name="codes", bufs=AHEAD + 2))
         work = stack.enter_context(tc.tile_pool(name="work", bufs=4))
         k_pool = stack.enter_context(tc.tile_pool(name="k", bufs=2 * H_TILES))
         sorted_pool = stack.enter_context(tc.tile_pool(name="sorted", bufs=2 * BLOCKS_PER_CHUNK))
-        psum = stack.enter_context(tc.psum_pool(name="psum", bufs=8))
+        psum = stack.enter_context(tc.psum_pool(name="psum", bufs=1))
 
         bias_rows = const.tile([P, P], BF16)
         nc.vector.memset(bias_rows[:], 0.0)
         w_planes = const.tile([P, 2, PASSES, CHAN], U8, align_bytes=256)
         nc.vector.memset(w_planes[:].rearrange("p w g n -> p (w g n)").bitcast(I32), 0)
-        sums = const.tile([P, P], F32)
-        nc.vector.memset(sums[:], 0.0)
+        parts = const.tile([P, TERMS, P], F32)
+        nc.vector.memset(parts[:].rearrange("p t c -> p (t c)"), 0.0)
         ident = const.tile([P, P], F32)
         make_identity(nc, ident[:])
         warm = const.tile([P, 1], F32)
-        nc.scalar.activation(out=warm[:], in_=sums[:, 0:1], func=ACT.Exp)
+        nc.scalar.activation(out=warm[:], in_=parts[:, 0, P - 1 : P], func=ACT.Exp)
 
         x_blocks_dram = x.rearrange("n (b p t) d -> (n b) p t d", p=P, t=TOKENS_PER_PARTITION)
         x_blocks = []
@@ -94,11 +94,14 @@ def tile_linearattention_pa_t_kernel(
         for b in range((AHEAD + 1) * BLOCKS_PER_CHUNK, CHUNKS * BLOCKS_PER_CHUNK):
             load_block(b)
 
-        parts = const.tile([P, TERMS, 2, BATCH, H_TILES], F32)
-        nc.vector.memset(parts[:].rearrange("p t s n j -> p (t s n j)"), 0.0)
+        def sum_column(which, n, j):
+            return (which * BATCH + n) * H_TILES + j
 
         def summed(c, j):
             return c >= CHUNKS - SUMMED_CHUNKS and j == H_TILES - 1
+        def bank(bank_set, i, shape, name):
+            return psum.tile(shape, F32, tag="bank%d" % (4 * bank_set + i), name=name)
+
         flipped = {}
         grouped = {}
         x_codes = {}
@@ -122,7 +125,7 @@ def tile_linearattention_pa_t_kernel(
             sort_block(c * BLOCKS_PER_CHUNK, nc.scalar.copy)
             sort_block(c * BLOCKS_PER_CHUNK + 1, nc.gpsimd.tensor_copy)
 
-        def transpose_chunk(c):
+        def transpose_chunk(c, bank_set):
             for blk in range(BLOCKS_PER_CHUNK):
                 b = c * BLOCKS_PER_CHUNK + blk
                 if b in sorted_words:
@@ -137,35 +140,49 @@ def tile_linearattention_pa_t_kernel(
                         .rearrange("p (t g q u) -> p t g u q", t=TOKENS_PER_PARTITION, g=PASSES, u=2)
                     )
                 for g in range(PASSES):
-                    bank = psum.tile([P, 2, TOKENS_PER_PARTITION, P], F32, tag="bank", name="flipped")
+                    quarter = blk * PASSES + g
+                    turned = bank(bank_set, quarter, [P, 2, TOKENS_PER_PARTITION, P], "flipped")
                     for u in range(2):
                         for t in range(TOKENS_PER_PARTITION):
-                            nc.tensor.transpose(bank[:, u, t, :], x_words[:, t, g, u, :], ident[:])
-                    flipped[c, blk * PASSES + g] = bank
+                            nc.tensor.transpose(turned[:, u, t, :], x_words[:, t, g, u, :], ident[:])
+                    flipped[c, quarter] = turned
 
         def copy_chunk(c):
+            laid = grouped_pool.tile([P, PASSES, BLOCKS_PER_CHUNK, 4 * BLOCK], BF16, align_bytes=64, tag="grouped", name="grouped")
             for quarter in range(QUARTERS):
-                laid = grouped_pool.tile([P, 4 * BLOCK], BF16, align_bytes=64, tag="grouped", name="grouped")
+                part = laid[:, quarter % PASSES, quarter // PASSES, :]
                 nc.scalar.copy(
-                    out=laid[:].bitcast(F32).rearrange("p (c u) -> p c u", u=2),
+                    out=part.bitcast(F32).rearrange("p (c u) -> p c u", u=2),
                     in_=flipped[c, quarter][:].rearrange("p u t r -> p (t r) u"),
                 )
-                grouped[c, quarter] = laid
+            grouped[c] = laid
 
         def quantise_chunk(c):
             codes = codes_pool.tile([P, PASSES, CHUNK], U32, align_bytes=256, tag="codes")
             scales = codes_pool.tile([P, PASSES, CHUNK], U8, align_bytes=256, tag="scales")
-            for quarter in range(QUARTERS):
-                blk, g = quarter // PASSES, quarter % PASSES
-                cols = slice(blk * BLOCK, (blk + 1) * BLOCK)
+            if c < AHEAD:
+                for quarter in range(QUARTERS):
+                    blk, g = quarter // PASSES, quarter % PASSES
+                    cols = slice(blk * BLOCK, (blk + 1) * BLOCK)
+                    nc.vector.quantize_mx(
+                        out=codes[:, g, cols].bitcast(FP8X4), scales=scales[:, g, cols], in_=grouped[c][:, g, blk, :]
+                    )
+            else:
                 nc.vector.quantize_mx(
-                    out=codes[:, g, cols].bitcast(FP8X4), scales=scales[:, g, cols], in_=grouped[c, quarter][:]
+                    out=codes[:].rearrange("p g n -> p (g n)").bitcast(FP8X4),
+                    scales=scales[:].rearrange("p g n -> p (g n)"),
+                    in_=grouped[c][:].rearrange("p g b n -> p (g b n)"),
                 )
             x_codes[c] = codes
             x_scales[c] = scales
 
+        def product_set(c, w):
+            if w == VALUE:
+                return c % 2 if c + AHEAD < CHUNKS else 1
+            return c % 2 if c + 1 < CHUNKS else 0
+
         def product(c, w, j):
-            acc = psum.tile([P, CHUNK], F32, tag="bank", name="acc")
+            acc = bank(product_set(c, w), j, [P, CHUNK], "acc")
             for g in range(PASSES):
                 nc.tensor.matmul_mx(
                     out=acc[:],
@@ -179,7 +196,8 @@ def tile_linearattention_pa_t_kernel(
             return acc
 
         def k_as_sum(c, j):
-            term, n = c % CHUNKS_PER_BATCH, c // CHUNKS_PER_BATCH
+            term = c % CHUNKS_PER_BATCH
+            column = sum_column(KSUM, c // CHUNKS_PER_BATCH, j)
             fallen = work.tile([P, CHUNK], F32, tag="fallen")
             nc.scalar.activation(
                 out=fallen[:],
@@ -195,35 +213,34 @@ def tile_linearattention_pa_t_kernel(
                 func=ACT.Relu,
                 bias=biases[:, j : j + 1],
                 scale=1.0,
-                accum_out=parts[:, CHUNKS_PER_BATCH + term, 1, n, j : j + 1],
+                accum_out=parts[:, CHUNKS_PER_BATCH + term, column : column + 1],
             )
             decayed = work.tile([P, CHUNK], F32, tag="decayed")
             nc.scalar.activation(
-                out=decayed[:], in_=fallen[:], func=ACT.Exp, scale=-1.0, accum_out=parts[:, term, 1, n, j : j + 1]
+                out=decayed[:], in_=fallen[:], func=ACT.Exp, scale=-1.0, accum_out=parts[:, term, column : column + 1]
             )
             k_tiles[c, j] = k_pool.tile([P, CHUNK], F32, tag="k", name="k")
             nc.gpsimd.tensor_tensor(out=k_tiles[c, j][:], in0=decayed[:], in1=ramp[:], op=ALU.add)
 
-        def keys(c):
-            for j in range(H_TILES):
-                key_accs[c, j] = product(c, KEY, j)
-            for j in range(H_TILES):
-                if summed(c, j):
-                    k_as_sum(c, j)
-                    continue
-                grown = work.tile([P, CHUNK], F32, tag="grown")
-                nc.scalar.activation(
-                    out=grown[:], in_=key_accs[c, j][:], func=ACT.Exp, bias=biases[:, j : j + 1], scale=1.0
-                )
-                clipped[c, j] = work.tile([P, CHUNK], F32, tag="clipped", name="clipped")
-                nc.gpsimd.tensor_scalar(
-                    out=clipped[c, j][:], in0=grown[:], scalar1=1.0, scalar2=0.0, op0=ALU.min, op1=ALU.max
-                )
+        def key_of(c, j):
+            key_accs[c, j] = product(c, KEY, j)
+            if summed(c, j):
+                k_as_sum(c, j)
+                return
+            grown = work.tile([P, CHUNK], F32, tag="grown")
+            nc.scalar.activation(
+                out=grown[:], in_=key_accs[c, j][:], func=ACT.Exp, bias=biases[:, j : j + 1], scale=1.0
+            )
+            clipped[c, j] = work.tile([P, CHUNK], F32, tag="clipped", name="clipped")
+            nc.gpsimd.tensor_scalar(
+                out=clipped[c, j][:], in0=grown[:], scalar1=1.0, scalar2=0.0, op0=ALU.min, op1=ALU.max
+            )
 
         def k_of(c, j):
             if summed(c, j):
                 return
             k_tiles[c, j] = k_pool.tile([P, CHUNK], F32, tag="k", name="k")
+            column = sum_column(KSUM, c // CHUNKS_PER_BATCH, j)
             nc.vector.scalar_tensor_tensor(
                 out=k_tiles[c, j][:],
                 in0=key_accs[c, j][:],
@@ -231,11 +248,12 @@ def tile_linearattention_pa_t_kernel(
                 in1=clipped[c, j][:],
                 op0=ALU.add,
                 op1=ALU.max,
-                accum_out=parts[:, c % CHUNKS_PER_BATCH, 1, c // CHUNKS_PER_BATCH, j : j + 1],
+                accum_out=parts[:, c % CHUNKS_PER_BATCH, column : column + 1],
             )
 
         def kv_of(c, j):
             kv_tile = work.tile([P, CHUNK], F32, tag="kv")
+            column = sum_column(KV, c // CHUNKS_PER_BATCH, j)
             nc.vector.scalar_tensor_tensor(
                 out=kv_tile[:],
                 in0=value_accs[c, j][:],
@@ -243,15 +261,12 @@ def tile_linearattention_pa_t_kernel(
                 in1=k_tiles[c, j][:],
                 op0=ALU.add,
                 op1=ALU.mult,
-                accum_out=parts[:, c % CHUNKS_PER_BATCH, 0, c // CHUNKS_PER_BATCH, j : j + 1],
+                accum_out=parts[:, c % CHUNKS_PER_BATCH, column : column + 1],
             )
 
         bias_rows_f32 = const.tile([P, P], F32)
         nc.vector.tensor_copy(out=bias_rows_f32[:], in_=bias_rows[:])
-        transpose_chunk(0)
-        copy_chunk(0)
-        quantise_chunk(0)
-        bias_flipped = psum.tile([P, P], F32, tag="bank")
+        bias_flipped = bank(1, 3, [P, P], "bias_flipped")
         nc.tensor.transpose(bias_flipped[:], bias_rows_f32[:], ident[:])
         biases = const.tile([P, 4 * H_TILES], F32)
         nc.vector.tensor_copy(out=biases[:, 0 : 2 * H_TILES], in_=bias_flipped[:, 0 : 2 * H_TILES])
@@ -261,31 +276,30 @@ def tile_linearattention_pa_t_kernel(
         nc.vector.tensor_scalar_mul(
             out=biases[:, 3 * H_TILES : 4 * H_TILES], in0=bias_flipped[:, 0:H_TILES], scalar1=-1.0
         )
-        for c in range(1, AHEAD):
-            transpose_chunk(c)
+        for c in range(AHEAD):
+            transpose_chunk(c, c % 2)
             copy_chunk(c)
             quantise_chunk(c)
         for blk in range(BLOCKS_PER_CHUNK):
             sort_block(AHEAD * BLOCKS_PER_CHUNK + blk, nc.vector.tensor_copy)
-        keys(0)
+        for j in range(H_TILES):
+            key_of(0, j)
         k_of(0, 0)
 
         for c in range(CHUNKS):
             if c + AHEAD < CHUNKS:
-                transpose_chunk(c + AHEAD)
+                transpose_chunk(c + AHEAD, (c + 1) % 2)
                 copy_chunk(c + AHEAD)
-            if c + AHEAD < CHUNKS:
                 for j in range(1, H_TILES):
                     k_of(c, j)
                 if c + AHEAD + 1 < CHUNKS:
                     sort_chunk(c + AHEAD + 1)
                 for j in range(H_TILES):
                     value_accs[c, j] = product(c, VALUE, j)
-                for j in range(H_TILES // 2):
+                    key_of(c + 1, j)
                     kv_of(c, j)
-                quantise_chunk(c + AHEAD)
-                for j in range(H_TILES // 2, H_TILES):
-                    kv_of(c, j)
+                    if j == 0:
+                        quantise_chunk(c + AHEAD)
             else:
                 value_accs[c, 0] = product(c, VALUE, 0)
                 for j in range(1, H_TILES):
@@ -293,16 +307,19 @@ def tile_linearattention_pa_t_kernel(
                     value_accs[c, j] = product(c, VALUE, j)
                     kv_of(c, j - 1)
                 kv_of(c, H_TILES - 1)
+                if c + 1 < CHUNKS:
+                    for j in range(H_TILES):
+                        key_of(c + 1, j)
             if c + 1 < CHUNKS:
-                keys(c + 1)
                 k_of(c + 1, 0)
 
         half = BATCH * H_TILES
-        nc.vector.tensor_reduce(
-            out=sums[:, 0 : 2 * half], in_=parts[:].rearrange("p t s n j -> p (s n j) t"), axis=AX.X, op=ALU.add
-        )
-        sums_flipped = psum.tile([P, P], F32, tag="bank")
-        nc.tensor.transpose(sums_flipped[:], sums[:], ident[:])
+        sums_flipped = bank(0, 0, [P, P], "sums_flipped")
+        order = (2, 0, 3, 1)
+        for t in order:
+            nc.tensor.matmul(
+                out=sums_flipped[:], lhsT=parts[:, t, :], rhs=ident[:], start=(t == order[0]), stop=(t == order[-1])
+            )
         rows_out = const.tile([P, P], F32)
         nc.vector.tensor_copy(out=rows_out[:], in_=sums_flipped[:])
         nc.sync.dma_start(out=out_0.rearrange("n (j p) -> (n j) p", p=P), in_=rows_out[0:half, :])

@@ -81,9 +81,10 @@ def tile_linearattention_pa_t_kernel(
             )
             return words
 
+        load_block(0)
         nc.sync.dma_start(out=bias_rows[0:H_TILES, :], in_=bk.rearrange("(j p) -> j p", p=P))
         nc.sync.dma_start(out=bias_rows[H_TILES : 2 * H_TILES, :], in_=bv.rearrange("(j p) -> j p", p=P))
-        for b in range(AHEAD * BLOCKS_PER_CHUNK):
+        for b in range(1, AHEAD * BLOCKS_PER_CHUNK):
             load_block(b)
         load_scales(KEY, Wk_scales)
         w_words = [load_words("wk_words", Wk_words)]
@@ -266,8 +267,11 @@ def tile_linearattention_pa_t_kernel(
 
         bias_rows_f32 = const.tile([P, P], F32)
         nc.vector.tensor_copy(out=bias_rows_f32[:], in_=bias_rows[:])
+        transpose_chunk(0, 0)
+        copy_chunk(0)
         bias_flipped = bank(1, 3, [P, P], "bias_flipped")
         nc.tensor.transpose(bias_flipped[:], bias_rows_f32[:], ident[:])
+        quantise_chunk(0)
         biases = const.tile([P, 4 * H_TILES], F32)
         nc.vector.tensor_copy(out=biases[:, 0 : 2 * H_TILES], in_=bias_flipped[:, 0 : 2 * H_TILES])
         nc.vector.tensor_scalar_add(
@@ -276,12 +280,11 @@ def tile_linearattention_pa_t_kernel(
         nc.vector.tensor_scalar_mul(
             out=biases[:, 3 * H_TILES : 4 * H_TILES], in0=bias_flipped[:, 0:H_TILES], scalar1=-1.0
         )
-        for c in range(AHEAD):
+        for c in range(1, AHEAD):
             transpose_chunk(c, c % 2)
             copy_chunk(c)
             quantise_chunk(c)
-        for blk in range(BLOCKS_PER_CHUNK):
-            sort_block(AHEAD * BLOCKS_PER_CHUNK + blk, nc.vector.tensor_copy)
+        sort_block(AHEAD * BLOCKS_PER_CHUNK, nc.vector.tensor_copy)
         for j in range(H_TILES):
             key_of(0, j)
         k_of(0, 0)

@@ -84,9 +84,10 @@ def tile_linearattention_pa_t_kernel(
         load_block(0)
         nc.sync.dma_start(out=bias_rows[0:H_TILES, :], in_=bk.rearrange("(j p) -> j p", p=P))
         nc.sync.dma_start(out=bias_rows[H_TILES : 2 * H_TILES, :], in_=bv.rearrange("(j p) -> j p", p=P))
-        for b in range(1, AHEAD * BLOCKS_PER_CHUNK):
-            load_block(b)
+        load_block(1)
         load_scales(KEY, Wk_scales)
+        for b in range(2, AHEAD * BLOCKS_PER_CHUNK):
+            load_block(b)
         w_words = [load_words("wk_words", Wk_words)]
         for b in range(AHEAD * BLOCKS_PER_CHUNK, (AHEAD + 1) * BLOCKS_PER_CHUNK):
             load_block(b)
@@ -126,8 +127,8 @@ def tile_linearattention_pa_t_kernel(
             sort_block(c * BLOCKS_PER_CHUNK, nc.scalar.copy)
             sort_block(c * BLOCKS_PER_CHUNK + 1, nc.gpsimd.tensor_copy)
 
-        def transpose_chunk(c, bank_set):
-            for blk in range(BLOCKS_PER_CHUNK):
+        def transpose_chunk(c, bank_set, blocks=range(BLOCKS_PER_CHUNK)):
+            for blk in blocks:
                 b = c * BLOCKS_PER_CHUNK + blk
                 if b in sorted_words:
                     x_words = sorted_words[b][:].rearrange(
@@ -267,11 +268,11 @@ def tile_linearattention_pa_t_kernel(
 
         bias_rows_f32 = const.tile([P, P], F32)
         nc.vector.tensor_copy(out=bias_rows_f32[:], in_=bias_rows[:])
-        transpose_chunk(0, 0)
-        copy_chunk(0)
+        transpose_chunk(0, 0, [0])
         bias_flipped = bank(1, 3, [P, P], "bias_flipped")
         nc.tensor.transpose(bias_flipped[:], bias_rows_f32[:], ident[:])
-        quantise_chunk(0)
+        transpose_chunk(0, 0, [1])
+        copy_chunk(0)
         biases = const.tile([P, 4 * H_TILES], F32)
         nc.vector.tensor_copy(out=biases[:, 0 : 2 * H_TILES], in_=bias_flipped[:, 0 : 2 * H_TILES])
         nc.vector.tensor_scalar_add(
@@ -280,6 +281,7 @@ def tile_linearattention_pa_t_kernel(
         nc.vector.tensor_scalar_mul(
             out=biases[:, 3 * H_TILES : 4 * H_TILES], in0=bias_flipped[:, 0:H_TILES], scalar1=-1.0
         )
+        quantise_chunk(0)
         for c in range(1, AHEAD):
             transpose_chunk(c, c % 2)
             copy_chunk(c)

@@ -81,13 +81,13 @@ def tile_linearattention_pa_t_kernel(
             )
             return words
 
-        load_block(0)
+        for b in range(BLOCKS_PER_CHUNK):
+            load_block(b)
+        load_scales(KEY, Wk_scales)
+        for b in range(BLOCKS_PER_CHUNK, AHEAD * BLOCKS_PER_CHUNK):
+            load_block(b)
         nc.sync.dma_start(out=bias_rows[0:H_TILES, :], in_=bk.rearrange("(j p) -> j p", p=P))
         nc.sync.dma_start(out=bias_rows[H_TILES : 2 * H_TILES, :], in_=bv.rearrange("(j p) -> j p", p=P))
-        load_block(1)
-        load_scales(KEY, Wk_scales)
-        for b in range(2, AHEAD * BLOCKS_PER_CHUNK):
-            load_block(b)
         w_words = [load_words("wk_words", Wk_words)]
         for b in range(AHEAD * BLOCKS_PER_CHUNK, (AHEAD + 1) * BLOCKS_PER_CHUNK):
             load_block(b)
@@ -127,8 +127,8 @@ def tile_linearattention_pa_t_kernel(
             sort_block(c * BLOCKS_PER_CHUNK, nc.scalar.copy)
             sort_block(c * BLOCKS_PER_CHUNK + 1, nc.gpsimd.tensor_copy)
 
-        def transpose_chunk(c, bank_set, blocks=range(BLOCKS_PER_CHUNK)):
-            for blk in blocks:
+        def transpose_chunk(c, bank_set):
+            for blk in range(BLOCKS_PER_CHUNK):
                 b = c * BLOCKS_PER_CHUNK + blk
                 if b in sorted_words:
                     x_words = sorted_words[b][:].rearrange(
@@ -159,24 +159,27 @@ def tile_linearattention_pa_t_kernel(
                 )
             grouped[c] = laid
 
-        def quantise_chunk(c):
-            codes = codes_pool.tile([P, PASSES, CHUNK], U32, align_bytes=256, tag="codes")
-            scales = codes_pool.tile([P, PASSES, CHUNK], U8, align_bytes=256, tag="scales")
-            if c < AHEAD:
-                for quarter in range(QUARTERS):
-                    blk, g = quarter // PASSES, quarter % PASSES
-                    cols = slice(blk * BLOCK, (blk + 1) * BLOCK)
-                    nc.vector.quantize_mx(
-                        out=codes[:, g, cols].bitcast(FP8X4), scales=scales[:, g, cols], in_=grouped[c][:, g, blk, :]
-                    )
-            else:
+        def code_tiles(c):
+            x_codes[c] = codes_pool.tile([P, PASSES, CHUNK], U32, align_bytes=256, tag="codes", name="codes")
+            x_scales[c] = codes_pool.tile([P, PASSES, CHUNK], U8, align_bytes=256, tag="scales", name="scales")
+
+        def quantise_quarters(c, quarters):
+            for quarter in quarters:
+                blk, g = quarter // PASSES, quarter % PASSES
+                cols = slice(blk * BLOCK, (blk + 1) * BLOCK)
                 nc.vector.quantize_mx(
-                    out=codes[:].rearrange("p g n -> p (g n)").bitcast(FP8X4),
-                    scales=scales[:].rearrange("p g n -> p (g n)"),
-                    in_=grouped[c][:].rearrange("p g b n -> p (g b n)"),
+                    out=x_codes[c][:, g, cols].bitcast(FP8X4),
+                    scales=x_scales[c][:, g, cols],
+                    in_=grouped[c][:, g, blk, :],
                 )
-            x_codes[c] = codes
-            x_scales[c] = scales
+
+        def quantise_chunk(c):
+            code_tiles(c)
+            nc.vector.quantize_mx(
+                out=x_codes[c][:].rearrange("p g n -> p (g n)").bitcast(FP8X4),
+                scales=x_scales[c][:].rearrange("p g n -> p (g n)"),
+                in_=grouped[c][:].rearrange("p g b n -> p (g b n)"),
+            )
 
         def product_set(c, w):
             if w == VALUE:
@@ -266,13 +269,18 @@ def tile_linearattention_pa_t_kernel(
                 accum_out=parts[:, c % CHUNKS_PER_BATCH, column : column + 1],
             )
 
+        transpose_chunk(0, 0)
+        copy_chunk(0)
+        code_tiles(0)
+        quantise_quarters(0, range(QUARTERS))
         bias_rows_f32 = const.tile([P, P], F32)
         nc.vector.tensor_copy(out=bias_rows_f32[:], in_=bias_rows[:])
-        transpose_chunk(0, 0, [0])
-        bias_flipped = bank(1, 3, [P, P], "bias_flipped")
+        transpose_chunk(1, 1)
+        copy_chunk(1)
+        bias_flipped = bank(0, H_TILES - 1, [P, P], "bias_flipped")
         nc.tensor.transpose(bias_flipped[:], bias_rows_f32[:], ident[:])
-        transpose_chunk(0, 0, [1])
-        copy_chunk(0)
+        code_tiles(1)
+        quantise_quarters(1, range(2))
         biases = const.tile([P, 4 * H_TILES], F32)
         nc.vector.tensor_copy(out=biases[:, 0 : 2 * H_TILES], in_=bias_flipped[:, 0 : 2 * H_TILES])
         nc.vector.tensor_scalar_add(
@@ -281,11 +289,7 @@ def tile_linearattention_pa_t_kernel(
         nc.vector.tensor_scalar_mul(
             out=biases[:, 3 * H_TILES : 4 * H_TILES], in0=bias_flipped[:, 0:H_TILES], scalar1=-1.0
         )
-        quantise_chunk(0)
-        for c in range(1, AHEAD):
-            transpose_chunk(c, c % 2)
-            copy_chunk(c)
-            quantise_chunk(c)
+        quantise_quarters(1, range(2, QUARTERS))
         sort_block(AHEAD * BLOCKS_PER_CHUNK, nc.vector.tensor_copy)
         for j in range(H_TILES):
             key_of(0, j)

@@ -31,8 +31,9 @@ FLOPS = 2 * BATCH * SEQ * FEAT * 2 * CHAN
 
 
 AHEAD = 2
-SUMMED_CHUNKS = 2
-TERMS = 2 * CHUNKS_PER_BATCH
+SUMMED_TILES = 2
+KEYS_AHEAD = 3
+TERMS = CHUNKS_PER_BATCH + 1
 
 
 def tile_linearattention_pa_t_kernel(
@@ -100,7 +101,7 @@ def tile_linearattention_pa_t_kernel(
             return (which * BATCH + n) * H_TILES + j
 
         def summed(c, j):
-            return c >= CHUNKS - SUMMED_CHUNKS and j == H_TILES - 1
+            return c == CHUNKS - 1 and j >= H_TILES - SUMMED_TILES
         def bank(bank_set, i, shape, name):
             return psum.tile(shape, F32, tag="bank%d" % (4 * bank_set + i), name=name)
 
@@ -181,13 +182,8 @@ def tile_linearattention_pa_t_kernel(
                 in_=grouped[c][:].rearrange("p g b n -> p (g b n)"),
             )
 
-        def product_set(c, w):
-            if w == VALUE:
-                return c % 2 if c + AHEAD < CHUNKS else 1
-            return c % 2 if c + 1 < CHUNKS else 0
-
         def product(c, w, j):
-            acc = bank(product_set(c, w), j, [P, CHUNK], "acc")
+            acc = bank(c % 2, j, [P, CHUNK], "acc")
             for g in range(PASSES):
                 nc.tensor.matmul_mx(
                     out=acc[:],
@@ -218,7 +214,7 @@ def tile_linearattention_pa_t_kernel(
                 func=ACT.Relu,
                 bias=biases[:, j : j + 1],
                 scale=1.0,
-                accum_out=parts[:, CHUNKS_PER_BATCH + term, column : column + 1],
+                accum_out=parts[:, CHUNKS_PER_BATCH, column : column + 1],
             )
             decayed = work.tile([P, CHUNK], F32, tag="decayed")
             nc.scalar.activation(
@@ -309,22 +305,27 @@ def tile_linearattention_pa_t_kernel(
                     kv_of(c, j)
                     if j == 0:
                         quantise_chunk(c + AHEAD)
-            else:
-                value_accs[c, 0] = product(c, VALUE, 0)
+            elif c + 1 < CHUNKS:
                 for j in range(1, H_TILES):
                     k_of(c, j)
+                for j in range(KEYS_AHEAD):
+                    key_of(c + 1, j)
+                for j in range(H_TILES):
                     value_accs[c, j] = product(c, VALUE, j)
-                    kv_of(c, j - 1)
-                kv_of(c, H_TILES - 1)
-                if c + 1 < CHUNKS:
-                    for j in range(H_TILES):
-                        key_of(c + 1, j)
-            if c + 1 < CHUNKS:
+                    if j + KEYS_AHEAD < H_TILES:
+                        key_of(c + 1, j + KEYS_AHEAD)
+                    kv_of(c, j)
+                    k_of(c + 1, j)
+            else:
+                for j in range(H_TILES):
+                    value_accs[c, j] = product(c, VALUE, j)
+                    kv_of(c, j)
+            if c + AHEAD < CHUNKS:
                 k_of(c + 1, 0)
 
         half = BATCH * H_TILES
         sums_flipped = bank(0, 0, [P, P], "sums_flipped")
-        order = (2, 0, 3, 1)
+        order = (0, 2, 1)
         for t in order:
             nc.tensor.matmul(
                 out=sums_flipped[:], lhsT=parts[:, t, :], rhs=ident[:], start=(t == order[0]), stop=(t == order[-1])

@@ -63,12 +63,12 @@ def tile_linearattention_pa_t_kernel(
         nc.scalar.activation(out=warm[:], in_=parts[:, 0, P - 1 : P], func=ACT.Exp)
 
         x_blocks_dram = x.rearrange("n (b p t) d -> (n b) p t d", p=P, t=TOKENS_PER_PARTITION)
-        x_blocks = []
+        x_blocks = {}
 
         def load_block(b):
             x_blk = x_pool.tile([P, TOKENS_PER_PARTITION, FEAT], BF16, tag="x")
             nc.sync.dma_start(out=x_blk[:], in_=x_blocks_dram[b])
-            x_blocks.append(x_blk)
+            x_blocks[b] = x_blk
 
         def load_scales(w, scales_dram):
             rows = scales_dram.rearrange("g (q r) n -> r q g n", r=4)
@@ -94,8 +94,9 @@ def tile_linearattention_pa_t_kernel(
             load_block(b)
         w_words.append(load_words("wv_words", Wv_words))
         load_scales(VALUE, Wv_scales)
-        for b in range((AHEAD + 1) * BLOCKS_PER_CHUNK, CHUNKS * BLOCKS_PER_CHUNK):
-            load_block(b)
+        for c in range(AHEAD + 1, CHUNKS):
+            load_block(c * BLOCKS_PER_CHUNK + 1)
+            load_block(c * BLOCKS_PER_CHUNK)
 
         def sum_column(which, n, j):
             return (which * BATCH + n) * H_TILES + j

from contextlib import ExitStack

import concourse.mybir as mybir
from concourse.masks import make_identity

F32 = mybir.dt.float32
BF16 = mybir.dt.bfloat16
I32 = mybir.dt.int32
U8 = mybir.dt.uint8
U32 = mybir.dt.uint32
FP8X4 = mybir.dt.float8_e4m3fn_x4
FP4X4 = mybir.dt.float4_e2m1fn_x4
ALU = mybir.AluOpType
ACT = mybir.ActivationFunctionType

P = 128
BATCH, SEQ, FEAT, CHAN = 4, 1024, 1024, 512
K_PASS = 4 * P
PASSES = FEAT // K_PASS
CHUNK = 512
CHUNKS = BATCH * SEQ // CHUNK
CHUNKS_PER_BATCH = SEQ // CHUNK
BLOCK = 256
BLOCKS_PER_CHUNK = CHUNK // BLOCK
TOKENS_PER_PARTITION = BLOCK // P
H_TILES = CHAN // P
KEY, VALUE = 0, 1
KV, KSUM = 0, 1

FLOPS = 2 * BATCH * SEQ * FEAT * 2 * CHAN


AHEAD = 2
SUMMED_TILES = 2
KEYS_AHEAD = 3
TERMS = CHUNKS_PER_BATCH + 1


def tile_linearattention_pa_t_kernel(
    tc, x, Wk_words, Wk_scales, bk, Wv_words, Wv_scales, bv, out_0, out_1
):
    nc = tc.nc
    with ExitStack() as stack:
        stack.enter_context(tc.manual_schedule())
        const = stack.enter_context(tc.tile_pool(name="const", bufs=1))
        x_pool = stack.enter_context(tc.tile_pool(name="x", bufs=CHUNKS * BLOCKS_PER_CHUNK))
        grouped_pool = stack.enter_context(tc.tile_pool(name="grouped", bufs=2))
        codes_pool = stack.enter_context(tc.tile_pool(name="codes", bufs=AHEAD + 2))
        work = stack.enter_context(tc.tile_pool(name="work", bufs=4))
        k_pool = stack.enter_context(tc.tile_pool(name="k", bufs=2 * H_TILES))
        sorted_pool = stack.enter_context(tc.tile_pool(name="sorted", bufs=2 * BLOCKS_PER_CHUNK))
        psum = stack.enter_context(tc.psum_pool(name="psum", bufs=1))

        bias_rows = const.tile([P, P], BF16)
        nc.vector.memset(bias_rows[:], 0.0)
        w_planes = const.tile([P, 2, PASSES, CHAN], U8, align_bytes=256)
        nc.vector.memset(w_planes[:].rearrange("p w g n -> p (w g n)").bitcast(I32), 0)
        parts = const.tile([P, TERMS, P], F32)
        nc.vector.memset(parts[:].rearrange("p t c -> p (t c)"), 0.0)
        ident = const.tile([P, P], F32)
        make_identity(nc, ident[:])
        warm = const.tile([P, 1], F32)
        nc.scalar.activation(out=warm[:], in_=parts[:, 0, P - 1 : P], func=ACT.Exp)

        x_blocks_dram = x.rearrange("n (b p t) d -> (n b) p t d", p=P, t=TOKENS_PER_PARTITION)
        x_blocks = {}

        def load_block(b):
            x_blk = x_pool.tile([P, TOKENS_PER_PARTITION, FEAT], BF16, tag="x")
            nc.sync.dma_start(out=x_blk[:], in_=x_blocks_dram[b])
            x_blocks[b] = x_blk

        def load_scales(w, scales_dram):
            rows = scales_dram.rearrange("g (q r) n -> r q g n", r=4)
            for r in range(4):
                nc.sync.dma_start(out=w_planes[r:P:32, w, :, :].bitcast(I32), in_=rows[r].bitcast(I32))

        def load_words(name, words_dram):
            words = const.tile([P, PASSES, 2 * CHAN], U8, align_bytes=256, name=name)
            nc.sync.dma_start(
                out=words[:].bitcast(I32), in_=words_dram.rearrange("g p b -> p g b").bitcast(I32)
            )
            return words

        for b in range(BLOCKS_PER_CHUNK):
            load_block(b)
        load_scales(KEY, Wk_scales)
        for b in range(BLOCKS_PER_CHUNK, AHEAD * BLOCKS_PER_CHUNK):
            load_block(b)
        nc.sync.dma_start(out=bias_rows[0:H_TILES, :], in_=bk.rearrange("(j p) -> j p", p=P))
        nc.sync.dma_start(out=bias_rows[H_TILES : 2 * H_TILES, :], in_=bv.rearrange("(j p) -> j p", p=P))
        w_words = [load_words("wk_words", Wk_words)]
        for b in range(AHEAD * BLOCKS_PER_CHUNK, (AHEAD + 1) * BLOCKS_PER_CHUNK):
            load_block(b)
        w_words.append(load_words("wv_words", Wv_words))
        load_scales(VALUE, Wv_scales)
        for c in range(AHEAD + 1, CHUNKS):
            load_block(c * BLOCKS_PER_CHUNK + 1)
            load_block(c * BLOCKS_PER_CHUNK)

        def sum_column(which, n, j):
            return (which * BATCH + n) * H_TILES + j

        def summed(c, j):
            return c == CHUNKS - 1 and j >= H_TILES - SUMMED_TILES
        def bank(bank_set, i, shape, name):
            return psum.tile(shape, F32, tag="bank%d" % (4 * bank_set + i), name=name)

        flipped = {}
        grouped = {}
        x_codes = {}
        x_scales = {}
        key_accs = {}
        value_accs = {}
        clipped = {}
        k_tiles = {}
        QUARTERS = BLOCKS_PER_CHUNK * PASSES

        sorted_words = {}

        def sort_block(b, copy):
            sorted_words[b] = sorted_pool.tile([P, BLOCK * FEAT // (2 * P)], F32, tag="sorted", name="sorted")
            copy(
                out=sorted_words[b][:].rearrange("p (a u q) -> p a u q", u=2, q=P),
                in_=x_blocks[b][:].rearrange("p t d -> p (t d)").bitcast(F32).rearrange("p (a q u) -> p a u q", u=2, q=P),
            )

        def sort_chunk(c):
            sort_block(c * BLOCKS_PER_CHUNK, nc.scalar.copy)
            sort_block(c * BLOCKS_PER_CHUNK + 1, nc.gpsimd.tensor_copy)

        def transpose_chunk(c, bank_set):
            for blk in range(BLOCKS_PER_CHUNK):
                b = c * BLOCKS_PER_CHUNK + blk
                if b in sorted_words:
                    x_words = sorted_words[b][:].rearrange(
                        "p (t g u q) -> p t g u q", t=TOKENS_PER_PARTITION, g=PASSES, u=2
                    )
                else:
                    x_words = (
                        x_blocks[b][:]
                        .rearrange("p t d -> p (t d)")
                        .bitcast(F32)
                        .rearrange("p (t g q u) -> p t g u q", t=TOKENS_PER_PARTITION, g=PASSES, u=2)
                    )
                for g in range(PASSES):
                    quarter = blk * PASSES + g
                    turned = bank(bank_set, quarter, [P, 2, TOKENS_PER_PARTITION, P], "flipped")
                    for u in range(2):
                        for t in range(TOKENS_PER_PARTITION):
                            nc.tensor.transpose(turned[:, u, t, :], x_words[:, t, g, u, :], ident[:])
                    flipped[c, quarter] = turned

        def copy_chunk(c):
            laid = grouped_pool.tile([P, PASSES, BLOCKS_PER_CHUNK, 4 * BLOCK], BF16, align_bytes=64, tag="grouped", name="grouped")
            for quarter in range(QUARTERS):
                part = laid[:, quarter % PASSES, quarter // PASSES, :]
                nc.scalar.copy(
                    out=part.bitcast(F32).rearrange("p (c u) -> p c u", u=2),
                    in_=flipped[c, quarter][:].rearrange("p u t r -> p (t r) u"),
                )
            grouped[c] = laid

        def code_tiles(c):
            x_codes[c] = codes_pool.tile([P, PASSES, CHUNK], U32, align_bytes=256, tag="codes", name="codes")
            x_scales[c] = codes_pool.tile([P, PASSES, CHUNK], U8, align_bytes=256, tag="scales", name="scales")

        def quantise_quarters(c, quarters):
            for quarter in quarters:
                blk, g = quarter // PASSES, quarter % PASSES
                cols = slice(blk * BLOCK, (blk + 1) * BLOCK)
                nc.vector.quantize_mx(
                    out=x_codes[c][:, g, cols].bitcast(FP8X4),
                    scales=x_scales[c][:, g, cols],
                    in_=grouped[c][:, g, blk, :],
                )

        def quantise_chunk(c):
            code_tiles(c)
            nc.vector.quantize_mx(
                out=x_codes[c][:].rearrange("p g n -> p (g n)").bitcast(FP8X4),
                scales=x_scales[c][:].rearrange("p g n -> p (g n)"),
                in_=grouped[c][:].rearrange("p g b n -> p (g b n)"),
            )

        def product(c, w, j):
            acc = bank(c % 2, j, [P, CHUNK], "acc")
            for g in range(PASSES):
                nc.tensor.matmul_mx(
                    out=acc[:],
                    lhsT=w_words[w][:, g, 2 * P * j : 2 * P * (j + 1)].bitcast(FP4X4),
                    lhsT_scale=w_planes[:, w, g, P * j : P * (j + 1)],
                    rhs=x_codes[c][:, g, :].bitcast(FP8X4),
                    rhs_scale=x_scales[c][:, g, :],
                    start=(g == 0),
                    stop=(g == PASSES - 1),
                )
            return acc

        def k_as_sum(c, j):
            term = c % CHUNKS_PER_BATCH
            column = sum_column(KSUM, c // CHUNKS_PER_BATCH, j)
            fallen = work.tile([P, CHUNK], F32, tag="fallen")
            nc.scalar.activation(
                out=fallen[:],
                in_=key_accs[c, j][:],
                func=ACT.Relu,
                bias=biases[:, 3 * H_TILES + j : 3 * H_TILES + j + 1],
                scale=-1.0,
            )
            ramp = work.tile([P, CHUNK], F32, tag="ramp")
            nc.scalar.activation(
                out=ramp[:],
                in_=key_accs[c, j][:],
                func=ACT.Relu,
                bias=biases[:, j : j + 1],
                scale=1.0,
                accum_out=parts[:, CHUNKS_PER_BATCH, column : column + 1],
            )
            decayed = work.tile([P, CHUNK], F32, tag="decayed")
            nc.scalar.activation(
                out=decayed[:], in_=fallen[:], func=ACT.Exp, scale=-1.0, accum_out=parts[:, term, column : column + 1]
            )
            k_tiles[c, j] = k_pool.tile([P, CHUNK], F32, tag="k", name="k")
            nc.gpsimd.tensor_tensor(out=k_tiles[c, j][:], in0=decayed[:], in1=ramp[:], op=ALU.add)

        def key_of(c, j):
            key_accs[c, j] = product(c, KEY, j)
            if summed(c, j):
                k_as_sum(c, j)
                return
            grown = work.tile([P, CHUNK], F32, tag="grown")
            nc.scalar.activation(
                out=grown[:], in_=key_accs[c, j][:], func=ACT.Exp, bias=biases[:, j : j + 1], scale=1.0
            )
            clipped[c, j] = work.tile([P, CHUNK], F32, tag="clipped", name="clipped")
            nc.gpsimd.tensor_scalar(
                out=clipped[c, j][:], in0=grown[:], scalar1=1.0, scalar2=0.0, op0=ALU.min, op1=ALU.max
            )

        def k_of(c, j):
            if summed(c, j):
                return
            k_tiles[c, j] = k_pool.tile([P, CHUNK], F32, tag="k", name="k")
            column = sum_column(KSUM, c // CHUNKS_PER_BATCH, j)
            nc.vector.scalar_tensor_tensor(
                out=k_tiles[c, j][:],
                in0=key_accs[c, j][:],
                scalar=biases[:, 2 * H_TILES + j : 2 * H_TILES + j + 1],
                in1=clipped[c, j][:],
                op0=ALU.add,
                op1=ALU.max,
                accum_out=parts[:, c % CHUNKS_PER_BATCH, column : column + 1],
            )

        def kv_of(c, j):
            kv_tile = work.tile([P, CHUNK], F32, tag="kv")
            column = sum_column(KV, c // CHUNKS_PER_BATCH, j)
            nc.vector.scalar_tensor_tensor(
                out=kv_tile[:],
                in0=value_accs[c, j][:],
                scalar=biases[:, H_TILES + j : H_TILES + j + 1],
                in1=k_tiles[c, j][:],
                op0=ALU.add,
                op1=ALU.mult,
                accum_out=parts[:, c % CHUNKS_PER_BATCH, column : column + 1],
            )

        transpose_chunk(0, 0)
        copy_chunk(0)
        code_tiles(0)
        quantise_quarters(0, range(QUARTERS))
        bias_rows_f32 = const.tile([P, P], F32)
        nc.vector.tensor_copy(out=bias_rows_f32[:], in_=bias_rows[:])
        transpose_chunk(1, 1)
        copy_chunk(1)
        bias_flipped = bank(0, H_TILES - 1, [P, P], "bias_flipped")
        nc.tensor.transpose(bias_flipped[:], bias_rows_f32[:], ident[:])
        code_tiles(1)
        quantise_quarters(1, range(2))
        biases = const.tile([P, 4 * H_TILES], F32)
        nc.vector.tensor_copy(out=biases[:, 0 : 2 * H_TILES], in_=bias_flipped[:, 0 : 2 * H_TILES])
        nc.vector.tensor_scalar_add(
            out=biases[:, 2 * H_TILES : 3 * H_TILES], in0=bias_flipped[:, 0:H_TILES], scalar1=1.0
        )
        nc.vector.tensor_scalar_mul(
            out=biases[:, 3 * H_TILES : 4 * H_TILES], in0=bias_flipped[:, 0:H_TILES], scalar1=-1.0
        )
        quantise_quarters(1, range(2, QUARTERS))
        sort_block(AHEAD * BLOCKS_PER_CHUNK, nc.vector.tensor_copy)
        for j in range(H_TILES):
            key_of(0, j)
        k_of(0, 0)

        for c in range(CHUNKS):
            if c + AHEAD < CHUNKS:
                transpose_chunk(c + AHEAD, (c + 1) % 2)
                copy_chunk(c + AHEAD)
                for j in range(1, H_TILES):
                    k_of(c, j)
                if c + AHEAD + 1 < CHUNKS:
                    sort_chunk(c + AHEAD + 1)
                for j in range(H_TILES):
                    value_accs[c, j] = product(c, VALUE, j)
                    key_of(c + 1, j)
                    kv_of(c, j)
                    if j == 0:
                        quantise_chunk(c + AHEAD)
            elif c + 1 < CHUNKS:
                for j in range(1, H_TILES):
                    k_of(c, j)
                for j in range(KEYS_AHEAD):
                    key_of(c + 1, j)
                for j in range(H_TILES):
                    value_accs[c, j] = product(c, VALUE, j)
                    if j + KEYS_AHEAD < H_TILES:
                        key_of(c + 1, j + KEYS_AHEAD)
                    kv_of(c, j)
                    k_of(c + 1, j)
            else:
                for j in range(H_TILES):
                    value_accs[c, j] = product(c, VALUE, j)
                    kv_of(c, j)
            if c + AHEAD < CHUNKS:
                k_of(c + 1, 0)

        half = BATCH * H_TILES
        sums_flipped = bank(0, 0, [P, P], "sums_flipped")
        order = (0, 2, 1)
        for t in order:
            nc.tensor.matmul(
                out=sums_flipped[:], lhsT=parts[:, t, :], rhs=ident[:], start=(t == order[0]), stop=(t == order[-1])
            )
        rows_out = const.tile([P, P], F32)
        nc.vector.tensor_copy(out=rows_out[:], in_=sums_flipped[:])
        nc.sync.dma_start(out=out_0.rearrange("n (j p) -> (n j) p", p=P), in_=rows_out[0:half, :])
        nc.scalar.dma_start(out=out_1.rearrange("n (j p) -> (n j) p", p=P), in_=rows_out[half : 2 * half, :])
